import numpy as np
import ml_dtypes


def mxq(x, axis, fmt="e4m3"):
    dtype, down = {"e4m3": (ml_dtypes.float8_e4m3fn, 7), "e5m2": (ml_dtypes.float8_e5m2, 14)}[fmt]
    v = np.moveaxis(np.asarray(x, np.float32).astype(ml_dtypes.bfloat16).astype(np.float64), axis, -1)
    blocks = v.reshape(v.shape[:-1] + (-1, 32))
    amax = np.abs(blocks).max(-1, keepdims=True)
    byte = np.maximum(np.where(amax > 0, np.frexp(amax)[1] - 1 + 127, 0) - down, 1)
    scale = np.exp2(byte - 127.0)
    codes = (blocks / scale).astype(np.float32).astype(dtype).astype(np.float64)
    return np.moveaxis((codes * scale).reshape(v.shape), -1, axis)


WIDE = False


def mx_kscale(k):
    if not WIDE:
        return np.ones(k)
    levels = np.array([10, -10, 5, -5, 0])
    if k % 512:
        return np.exp2(np.random.permutation(np.resize(levels, k // 32))).repeat(32)
    a = np.empty((k // 512, 16))
    for p in range(k // 512):
        a[p, :8] = np.random.permutation(np.resize(levels, 8))
        for g in range(8):
            far = levels[np.abs(levels - a[p, g]) >= 10]
            a[p, g + 8] = far[np.random.randint(len(far))]
    return np.exp2(a.ravel()).repeat(32)


BF16 = ml_dtypes.bfloat16


def bf(x):
    return np.asarray(x, np.float32).astype(BF16)


def f64(x):
    return np.asarray(x).astype(np.float64)


B, L, D, E, S = 2, 512, 1024, 2048, 128
F = E + E + S
LN_EPS = 1e-5
GQ = 1.75 * np.sqrt(np.sqrt(10.0 * L / S))


def silu(v):
    return v / (1.0 + np.exp(-v))


def setup_inputs():
    n = np.random.standard_normal
    s = mx_kscale(D)
    return {"x": bf(0.7 * n((B, L, D)) + 0.3 * n((B, L, 1))),
            "ln_g": bf((1.0 + 0.1 * n(D)) * s),
            "ln_b": bf(0.1 * n(D) * s),
            "W_in": bf(n((D, F)) / np.sqrt(D) / s[:, None]),
            "b_in": bf(0.2 * n(F)),
            "gamma_q": bf(GQ * (1.0 + 0.1 * n(S))),
            "beta_q": bf(GQ * (-0.2 + 0.1 * n(S))),
            "gamma_k": bf(GQ * (1.0 + 0.1 * n(S))),
            "beta_k": bf(GQ * (-0.2 + 0.1 * n(S)))}


def reference(x, ln_g, ln_b, W_in, b_in, gamma_q, beta_q, gamma_k, beta_k):
    x = f64(x)
    mu = x.mean(-1, keepdims=True)
    var = np.square(x - mu).mean(-1, keepdims=True)
    xn = (x - mu) / np.sqrt(var + LN_EPS) * f64(ln_g) + f64(ln_b)
    uvz = silu((mxq(xn, 2, "e4m3") @ mxq(f64(W_in), 0, "e4m3")) + f64(b_in))
    u, v, z = uvz[..., :E], uvz[..., E:E + E], uvz[..., E + E:]
    q = z * f64(gamma_q) + f64(beta_q)
    k = z * f64(gamma_k) + f64(beta_k)
    return u, v, q, k

@@ -1,0 +1,258 @@
+from contextlib import ExitStack
+
+import concourse.mybir as mybir
+from concourse.masks import make_identity
+
+F32 = mybir.dt.float32
+BF16 = mybir.dt.bfloat16
+U32 = mybir.dt.uint32
+U8 = mybir.dt.uint8
+FP8X4 = mybir.dt.float8_e4m3fn_x4
+ALU = mybir.AluOpType
+ACT = mybir.ActivationFunctionType
+
+P = 128
+PACK = 4
+PASSES = 2
+ROWS = 1024
+D = 1024
+E = 2048
+S = 128
+F = E + E + S
+ROW_TILES = ROWS // P
+PAIRS = ROW_TILES // 2
+K_TILES = D // P
+BANK = 512
+CHUNK = 1024
+CHUNKS = (E + E) // CHUNK
+LN_EPS = 1e-5
+FLOPS = 2 * ROWS * D * F
+
+
+def tile_gaublock_pb_kernel(
+    tc, x, ln_g, ln_b, W_in, b_in, gamma_q, beta_q, gamma_k, beta_k, out_0, out_1, out_2, out_3
+):
+    nc = tc.nc
+    x_rows = x.flatten_outer_dims().rearrange("(p m) k -> p m k", m=ROW_TILES)
+    w_rows = W_in.rearrange("(c p t) n -> p c t n", p=P, t=PACK)
+    uv_rows = [out.flatten_outer_dims().rearrange("(p m) f -> p m f", m=ROW_TILES) for out in (out_0, out_1)]
+    qk_rows = [out.flatten_outer_dims().rearrange("(p m) s -> p m s", m=ROW_TILES) for out in (out_2, out_3)]
+
+    with ExitStack() as ctx:
+        keep = ctx.enter_context(tc.tile_pool(name="keep", bufs=1))
+        stat = ctx.enter_context(tc.tile_pool(name="stat", bufs=2))
+        normed = ctx.enter_context(tc.tile_pool(name="normed", bufs=4))
+        stage = ctx.enter_context(tc.tile_pool(name="stage", bufs=2))
+        result = ctx.enter_context(tc.tile_pool(name="result", bufs=4))
+        psum = ctx.enter_context(tc.psum_pool(name="psum", bufs=8))
+
+        g_raw = keep.tile([P, PASSES, PACK], BF16, name="g_raw")
+        b_raw = keep.tile([P, PASSES, PACK], BF16, name="b_raw")
+        nc.scalar.dma_start(out=g_raw[:], in_=ln_g.rearrange("(c p t) -> p c t", p=P, t=PACK))
+        nc.scalar.dma_start(out=b_raw[:], in_=ln_b.rearrange("(c p t) -> p c t", p=P, t=PACK))
+        minus_half = keep.tile([P, 2], F32, name="minus_half")
+        nc.vector.memset(minus_half[:], -0.5)
+        ident_f32 = keep.tile([P, P], F32, name="ident_f32")
+        make_identity(nc, ident_f32[:])
+
+        x_sb = keep.tile([P, ROW_TILES, D], BF16, name="x_sb")
+        w_raw = {}
+        bias_all = keep.tile([P, F], BF16, name="bias_all")
+        qk_all = keep.tile([P, 4, S], BF16, name="qk_all")
+        wz_raw = keep.tile([P, PASSES, PACK, S], BF16, name="wz_raw")
+
+        def load_x(pair):
+            nc.sync.dma_start(out=x_sb[:, 2 * pair : 2 * pair + 2, :], in_=x_rows[:, 2 * pair : 2 * pair + 2, :])
+
+        def load_w(chunk):
+            for c in range(PASSES):
+                raw = keep.tile([P, PACK, CHUNK], BF16, name="w_raw%d_%d" % (chunk, c))
+                nc.sync.dma_start(
+                    out=raw[:], in_=w_rows[:, c, :, CHUNK * chunk : CHUNK * (chunk + 1)]
+                )
+                w_raw[(chunk, c)] = raw
+
+        load_x(0)
+        load_x(1)
+        load_w(0)
+        load_x(2)
+        load_x(3)
+        nc.sync.dma_start(out=bias_all[:], in_=b_in.partition_broadcast(P))
+        for chunk in range(1, CHUNKS):
+            load_w(chunk)
+        for c in range(PASSES):
+            nc.sync.dma_start(out=wz_raw[:, c, :, :], in_=w_rows[:, c, :, 2 * E : F])
+        for i, vec in enumerate((gamma_q, beta_q, gamma_k, beta_k)):
+            nc.sync.dma_start(out=qk_all[:, i, :], in_=vec.partition_broadcast(P))
+
+        g_cols = keep.tile([P, K_TILES], F32, name="g_cols")
+        b_cols = keep.tile([P, K_TILES], F32, name="b_cols")
+        nc.vector.tensor_copy(out=g_cols[:], in_=g_raw[:].rearrange("p c t -> p (c t)"))
+        nc.vector.tensor_copy(out=b_cols[:], in_=b_raw[:].rearrange("p c t -> p (c t)"))
+
+        xn_codes = keep.tile([P, PAIRS, PASSES, 2 * P], U32, name="xn_codes", align_bytes=64)
+        xn_scales = keep.tile([P, PAIRS, PASSES, 2 * P], U8, name="xn_scales", align_bytes=64)
+        w_codes = keep.tile([P, PASSES, 2 * E], U32, name="w_codes", align_bytes=64)
+        w_scales = keep.tile([P, PASSES, 2 * E], U8, name="w_scales", align_bytes=64)
+        wz_codes = keep.tile([P, PASSES, S], U32, name="wz_codes", align_bytes=64)
+        wz_scales = keep.tile([P, PASSES, S], U8, name="wz_scales", align_bytes=64)
+
+        def regroup(copy, dst, src):
+            copy(
+                out=dst.rearrange("p (a i) t -> p a t i", i=4),
+                in_=src.rearrange("p t (a i) -> p a t i", i=4),
+            )
+
+        def layer_norm(pair):
+            stats = stat.tile([P, 2, 2, 6], F32, name="stats")
+            mean_var = stat.tile([P, 2, 2], F32, name="mean_var")
+            for i in range(2):
+                for h in range(2):
+                    nc.vector.bn_stats(out=stats[:, i, h, :], in_=x_sb[:, 2 * pair + i, 512 * h : 512 * (h + 1)])
+                nc.vector.bn_aggr(out=mean_var[:, i, :], in_=stats[:, i, :, :].rearrange("p a b -> p (a b)"))
+            var_eps = stat.tile([P, 2], F32, name="var_eps")
+            nc.vector.tensor_scalar_add(out=var_eps[:], in0=mean_var[:, :, 1], scalar1=LN_EPS)
+            neg_mean = stat.tile([P, 2], F32, name="neg_mean")
+            nc.vector.tensor_scalar_mul(out=neg_mean[:], in0=mean_var[:, :, 0], scalar1=-1.0)
+            rstd = stat.tile([P, 2], F32, name="rstd")
+            nc.gpsimd.tensor_tensor(out=rstd[:], in0=var_eps[:], in1=minus_half[:], op=ALU.pow)
+            rows = []
+            for i in range(2):
+                y = normed.tile([P, PASSES, PACK, P], F32, name="y")
+                nc.gpsimd.tensor_scalar(
+                    out=y[:],
+                    in0=x_sb[:, 2 * pair + i, :].rearrange("p (c q t) -> p c t q", c=PASSES, t=PACK),
+                    scalar1=neg_mean[:, i : i + 1],
+                    scalar2=rstd[:, i : i + 1],
+                    op0=ALU.add,
+                    op1=ALU.mult,
+                )
+                rows.append(y)
+            k_tiles = stage.tile([P, K_TILES, 2 * P], BF16, name="k_tiles")
+            for a in range(K_TILES // 2):
+                turned = psum.tile([P, 2, 2 * P], F32, name="turned", tag="bank")
+                for b in range(2):
+                    j = 2 * a + b
+                    for i in range(2):
+                        nc.tensor.transpose(
+                            out=turned[:, b, P * i : P * (i + 1)], in_=rows[i][:, j // PACK, j % PACK, :], identity=ident_f32[:]
+                        )
+                for b in range(2):
+                    j = 2 * a + b
+                    nc.scalar.activation(
+                        out=k_tiles[:, j, :],
+                        in_=turned[:, b, :],
+                        func=ACT.Identity,
+                        scale=g_cols[:, j : j + 1],
+                        bias=b_cols[:, j : j + 1],
+                    )
+            grouped = stage.tile([P, PASSES, 2 * P, PACK], BF16, name="xn_grouped", align_bytes=64)
+            for c in range(PASSES):
+                regroup(nc.scalar.copy, grouped[:, c, :, :], k_tiles[:, PACK * c : PACK * (c + 1), :])
+            nc.vector.quantize_mx(
+                out=xn_codes[:, pair, :, :].rearrange("p c r -> p (c r)").bitcast(FP8X4),
+                scales=xn_scales[:, pair, :, :].rearrange("p c r -> p (c r)"),
+                in_=grouped[:].rearrange("p c r t -> p (c r t)"),
+            )
+
+        def quantise_w(chunk):
+            cols = slice(CHUNK * chunk, CHUNK * (chunk + 1))
+            grouped = []
+            for c, copy in enumerate((nc.vector.tensor_copy, nc.scalar.copy)):
+                g = stage.tile([P, CHUNK, PACK], BF16, name="w_grouped", align_bytes=64)
+                regroup(copy, g[:], w_raw[(chunk, c)][:])
+                grouped.append(g)
+            for c in range(PASSES):
+                nc.vector.quantize_mx(
+                    out=w_codes[:, c, cols].bitcast(FP8X4),
+                    scales=w_scales[:, c, cols],
+                    in_=grouped[c][:].rearrange("p n t -> p (n t)"),
+                )
+
+        def quantise_wz():
+            grouped = keep.tile([P, PASSES, S, PACK], BF16, name="wz_grouped", align_bytes=64)
+            for c in range(PASSES):
+                regroup(nc.scalar.copy, grouped[:, c, :, :], wz_raw[:, c, :, :])
+            nc.vector.quantize_mx(
+                out=wz_codes[:].rearrange("p c n -> p (c n)").bitcast(FP8X4),
+                scales=wz_scales[:].rearrange("p c n -> p (c n)"),
+                in_=grouped[:].rearrange("p c n t -> p (c n t)"),
+            )
+
+        def mx_group(acc, tile_m, rhs_codes, rhs_scales):
+            pair, i = tile_m // 2, tile_m % 2
+            for c in range(PASSES):
+                nc.tensor.matmul_mx(
+                    out=acc,
+                    lhsT=xn_codes[:, pair, c, P * i : P * (i + 1)].bitcast(FP8X4),
+                    lhsT_scale=xn_scales[:, pair, c, P * i : P * (i + 1)],
+                    rhs=rhs_codes[c].bitcast(FP8X4),
+                    rhs_scale=rhs_scales[c],
+                    start=(c == 0),
+                    stop=(c == PASSES - 1),
+                )
+
+        def project(chunk, pair):
+            out_sb = result.tile([P, 2, CHUNK], F32, name="out_sb")
+            for i in range(2):
+                for h in range(CHUNK // BANK):
+                    cols = slice(CHUNK * chunk + BANK * h, CHUNK * chunk + BANK * (h + 1))
+                    acc = psum.tile([P, BANK], F32, name="acc", tag="bank")
+                    mx_group(
+                        acc[:],
+                        2 * pair + i,
+                        [w_codes[:, c, cols] for c in range(PASSES)],
+                        [w_scales[:, c, cols] for c in range(PASSES)],
+                    )
+                    nc.vector.tensor_tensor(
+                        out=out_sb[:, i, BANK * h : BANK * (h + 1)], in0=acc[:], in1=bias_all[:, cols], op=ALU.add
+                    )
+            nc.scalar.activation(out=out_sb[:], in_=out_sb[:], func=ACT.Silu)
+            first = (CHUNK * chunk) % E
+            nc.sync.dma_start(
+                out=uv_rows[(CHUNK * chunk) // E][:, 2 * pair : 2 * pair + 2, first : first + CHUNK], in_=out_sb[:]
+            )
+
+        def project_z():
+            z_sb = result.tile([P, ROW_TILES, S], F32, name="z_sb", tag="out_sb")
+            per_bank = BANK // S
+            for a in range(ROW_TILES // per_bank):
+                acc = psum.tile([P, per_bank, S], F32, name="acc_z", tag="bank")
+                for i in range(per_bank):
+                    mx_group(
+                        acc[:, i, :],
+                        per_bank * a + i,
+                        [wz_codes[:, c, :] for c in range(PASSES)],
+                        [wz_scales[:, c, :] for c in range(PASSES)],
+                    )
+                nc.vector.tensor_tensor(
+                    out=z_sb[:, per_bank * a : per_bank * (a + 1), :],
+                    in0=acc[:],
+                    in1=bias_all[:, 2 * E : F].unsqueeze(1).to_broadcast([P, per_bank, S]),
+                    op=ALU.add,
+                )
+            nc.scalar.activation(out=z_sb[:], in_=z_sb[:], func=ACT.Silu)
+            for w in range(2):
+                gain = qk_all[:, 2 * w, :].unsqueeze(1).to_broadcast([P, ROW_TILES, S])
+                offset = qk_all[:, 2 * w + 1, :].unsqueeze(1).to_broadcast([P, ROW_TILES, S])
+                mapped = result.tile([P, ROW_TILES, S], F32, name="mapped", tag="out_sb")
+                nc.gpsimd.tensor_tensor(out=mapped[:], in0=z_sb[:], in1=gain, op=ALU.mult)
+                nc.gpsimd.tensor_tensor(out=mapped[:], in0=mapped[:], in1=offset, op=ALU.add)
+                nc.sync.dma_start(out=qk_rows[w], in_=mapped[:])
+
+        layer_norm(0)
+        quantise_w(0)
+        for pair in range(PAIRS):
+            if pair + 1 < PAIRS:
+                layer_norm(pair + 1)
+            else:
+                quantise_w(1)
+            project(0, pair)
+        for chunk in range(1, CHUNKS):
+            if chunk + 1 < CHUNKS:
+                quantise_w(chunk + 1)
+            else:
+                quantise_wz()
+                project_z()
+            for pair in range(PAIRS):
+                project(chunk, pair)

@@ -42,9 +42,12 @@ def tile_gaublock_pb_kernel(
         keep = ctx.enter_context(tc.tile_pool(name="keep", bufs=1))
         stat = ctx.enter_context(tc.tile_pool(name="stat", bufs=2))
         normed = ctx.enter_context(tc.tile_pool(name="normed", bufs=4))
+        raw = ctx.enter_context(tc.tile_pool(name="raw", bufs=6))
         stage = ctx.enter_context(tc.tile_pool(name="stage", bufs=2))
+        wstage = ctx.enter_context(tc.tile_pool(name="wstage", bufs=3))
         result = ctx.enter_context(tc.tile_pool(name="result", bufs=4))
         psum = ctx.enter_context(tc.psum_pool(name="psum", bufs=8))
+        ctx.enter_context(tc.manual_schedule())
 
         g_raw = keep.tile([P, PASSES, PACK], BF16, name="g_raw")
         b_raw = keep.tile([P, PASSES, PACK], BF16, name="b_raw")
@@ -52,48 +55,41 @@ def tile_gaublock_pb_kernel(
         nc.scalar.dma_start(out=b_raw[:], in_=ln_b.rearrange("(c p t) -> p c t", p=P, t=PACK))
         minus_half = keep.tile([P, 2], F32, name="minus_half")
         nc.vector.memset(minus_half[:], -0.5)
-        ident_f32 = keep.tile([P, P], F32, name="ident_f32")
-        make_identity(nc, ident_f32[:])
+        ident = keep.tile([P, P], F32, name="ident")
+        make_identity(nc, ident[:])
 
         x_sb = keep.tile([P, ROW_TILES, D], BF16, name="x_sb")
-        w_raw = {}
         bias_all = keep.tile([P, F], BF16, name="bias_all")
         qk_all = keep.tile([P, 4, S], BF16, name="qk_all")
         wz_raw = keep.tile([P, PASSES, PACK, S], BF16, name="wz_raw")
+        w_raw = {}
 
         def load_x(pair):
             nc.sync.dma_start(out=x_sb[:, 2 * pair : 2 * pair + 2, :], in_=x_rows[:, 2 * pair : 2 * pair + 2, :])
 
-        def load_w(chunk):
-            for c in range(PASSES):
-                raw = keep.tile([P, PACK, CHUNK], BF16, name="w_raw%d_%d" % (chunk, c))
-                nc.sync.dma_start(
-                    out=raw[:], in_=w_rows[:, c, :, CHUNK * chunk : CHUNK * (chunk + 1)]
-                )
-                w_raw[(chunk, c)] = raw
+        def load_w(chunk, c):
+            w_raw[(chunk, c)] = raw.tile([P, PACK, CHUNK], BF16, name="w_raw")
+            nc.sync.dma_start(out=w_raw[(chunk, c)][:], in_=w_rows[:, c, :, CHUNK * chunk : CHUNK * (chunk + 1)])
 
         load_x(0)
+        load_w(0, 0)
         load_x(1)
-        load_w(0)
+        load_w(0, 1)
         load_x(2)
         load_x(3)
         nc.sync.dma_start(out=bias_all[:], in_=b_in.partition_broadcast(P))
-        for chunk in range(1, CHUNKS):
-            load_w(chunk)
+        for chunk in range(1, CHUNKS - 1):
+            for c in range(PASSES):
+                load_w(chunk, c)
         for c in range(PASSES):
             nc.sync.dma_start(out=wz_raw[:, c, :, :], in_=w_rows[:, c, :, 2 * E : F])
         for i, vec in enumerate((gamma_q, beta_q, gamma_k, beta_k)):
             nc.sync.dma_start(out=qk_all[:, i, :], in_=vec.partition_broadcast(P))
 
-        g_cols = keep.tile([P, K_TILES], F32, name="g_cols")
-        b_cols = keep.tile([P, K_TILES], F32, name="b_cols")
-        nc.vector.tensor_copy(out=g_cols[:], in_=g_raw[:].rearrange("p c t -> p (c t)"))
-        nc.vector.tensor_copy(out=b_cols[:], in_=b_raw[:].rearrange("p c t -> p (c t)"))
-
         xn_codes = keep.tile([P, PAIRS, PASSES, 2 * P], U32, name="xn_codes", align_bytes=64)
         xn_scales = keep.tile([P, PAIRS, PASSES, 2 * P], U8, name="xn_scales", align_bytes=64)
-        w_codes = keep.tile([P, PASSES, 2 * E], U32, name="w_codes", align_bytes=64)
-        w_scales = keep.tile([P, PASSES, 2 * E], U8, name="w_scales", align_bytes=64)
+        w_codes = keep.tile([P, 2 * E // BANK, PASSES, BANK], U32, name="w_codes", align_bytes=64)
+        w_scales = keep.tile([P, 2 * E // BANK, PASSES, BANK], U8, name="w_scales", align_bytes=64)
         wz_codes = keep.tile([P, PASSES, S], U32, name="wz_codes", align_bytes=64)
         wz_scales = keep.tile([P, PASSES, S], U8, name="wz_scales", align_bytes=64)
 
@@ -103,80 +99,81 @@ def tile_gaublock_pb_kernel(
                 in_=src.rearrange("p t (a i) -> p a t i", i=4),
             )
 
-        def layer_norm(pair):
+        y_rows, k_tiles, xn_grouped, w_grouped = {}, {}, {}, {}
+
+        def normalise(pair):
             stats = stat.tile([P, 2, 2, 6], F32, name="stats")
             mean_var = stat.tile([P, 2, 2], F32, name="mean_var")
             for i in range(2):
                 for h in range(2):
                     nc.vector.bn_stats(out=stats[:, i, h, :], in_=x_sb[:, 2 * pair + i, 512 * h : 512 * (h + 1)])
+            for i in range(2):
                 nc.vector.bn_aggr(out=mean_var[:, i, :], in_=stats[:, i, :, :].rearrange("p a b -> p (a b)"))
             var_eps = stat.tile([P, 2], F32, name="var_eps")
-            nc.vector.tensor_scalar_add(out=var_eps[:], in0=mean_var[:, :, 1], scalar1=LN_EPS)
-            neg_mean = stat.tile([P, 2], F32, name="neg_mean")
-            nc.vector.tensor_scalar_mul(out=neg_mean[:], in0=mean_var[:, :, 0], scalar1=-1.0)
+            nc.gpsimd.tensor_scalar_add(out=var_eps[:], in0=mean_var[:, :, 1], scalar1=LN_EPS)
             rstd = stat.tile([P, 2], F32, name="rstd")
             nc.gpsimd.tensor_tensor(out=rstd[:], in0=var_eps[:], in1=minus_half[:], op=ALU.pow)
-            rows = []
             for i in range(2):
                 y = normed.tile([P, PASSES, PACK, P], F32, name="y")
                 nc.gpsimd.tensor_scalar(
                     out=y[:],
                     in0=x_sb[:, 2 * pair + i, :].rearrange("p (c q t) -> p c t q", c=PASSES, t=PACK),
-                    scalar1=neg_mean[:, i : i + 1],
+                    scalar1=mean_var[:, i, 0:1],
                     scalar2=rstd[:, i : i + 1],
-                    op0=ALU.add,
+                    op0=ALU.subtract,
                     op1=ALU.mult,
                 )
-                rows.append(y)
-            k_tiles = stage.tile([P, K_TILES, 2 * P], BF16, name="k_tiles")
+                y_rows[(pair, i)] = y
+
+        def turn(pair):
+            k_tiles[pair] = stage.tile([P, K_TILES, 2 * P], BF16, name="k_tiles")
             for a in range(K_TILES // 2):
                 turned = psum.tile([P, 2, 2 * P], F32, name="turned", tag="bank")
                 for b in range(2):
                     j = 2 * a + b
                     for i in range(2):
                         nc.tensor.transpose(
-                            out=turned[:, b, P * i : P * (i + 1)], in_=rows[i][:, j // PACK, j % PACK, :], identity=ident_f32[:]
+                            out=turned[:, b, P * i : P * (i + 1)],
+                            in_=y_rows[(pair, i)][:, j // PACK, j % PACK, :],
+                            identity=ident[:],
                         )
                 for b in range(2):
                     j = 2 * a + b
                     nc.scalar.activation(
-                        out=k_tiles[:, j, :],
+                        out=k_tiles[pair][:, j, :],
                         in_=turned[:, b, :],
                         func=ACT.Identity,
                         scale=g_cols[:, j : j + 1],
                         bias=b_cols[:, j : j + 1],
                     )
-            grouped = stage.tile([P, PASSES, 2 * P, PACK], BF16, name="xn_grouped", align_bytes=64)
+
+        def group_x(pair):
+            xn_grouped[pair] = stage.tile([P, PASSES, 2 * P, PACK], BF16, name="xn_grouped", align_bytes=64)
             for c in range(PASSES):
-                regroup(nc.scalar.copy, grouped[:, c, :, :], k_tiles[:, PACK * c : PACK * (c + 1), :])
+                regroup(
+                    nc.vector.tensor_copy,
+                    xn_grouped[pair][:, c, :, :],
+                    k_tiles[pair][:, PACK * c : PACK * (c + 1), :],
+                )
+
+        def quantise_x(pair):
             nc.vector.quantize_mx(
                 out=xn_codes[:, pair, :, :].rearrange("p c r -> p (c r)").bitcast(FP8X4),
                 scales=xn_scales[:, pair, :, :].rearrange("p c r -> p (c r)"),
-                in_=grouped[:].rearrange("p c r t -> p (c r t)"),
+                in_=xn_grouped[pair][:].rearrange("p c r t -> p (c r t)"),
             )
 
-        def quantise_w(chunk):
-            cols = slice(CHUNK * chunk, CHUNK * (chunk + 1))
-            grouped = []
-            for c, copy in enumerate((nc.vector.tensor_copy, nc.scalar.copy)):
-                g = stage.tile([P, CHUNK, PACK], BF16, name="w_grouped", align_bytes=64)
-                regroup(copy, g[:], w_raw[(chunk, c)][:])
-                grouped.append(g)
-            for c in range(PASSES):
-                nc.vector.quantize_mx(
-                    out=w_codes[:, c, cols].bitcast(FP8X4),
-                    scales=w_scales[:, c, cols],
-                    in_=grouped[c][:].rearrange("p n t -> p (n t)"),
-                )
+        def group_w(bank, c, copy):
+            if bank not in w_grouped:
+                w_grouped[bank] = wstage.tile([P, PASSES, BANK, PACK], BF16, name="w_grouped", align_bytes=64)
+            chunk, h = divmod(bank, CHUNK // BANK)
+            regroup(copy, w_grouped[bank][:, c, :, :], w_raw[(chunk, c)][:, :, BANK * h : BANK * (h + 1)])
 
-        def quantise_wz():
-            grouped = keep.tile([P, PASSES, S, PACK], BF16, name="wz_grouped", align_bytes=64)
-            for c in range(PASSES):
-                regroup(nc.scalar.copy, grouped[:, c, :, :], wz_raw[:, c, :, :])
+        def quantise_w(bank):
             nc.vector.quantize_mx(
-                out=wz_codes[:].rearrange("p c n -> p (c n)").bitcast(FP8X4),
-                scales=wz_scales[:].rearrange("p c n -> p (c n)"),
-                in_=grouped[:].rearrange("p c n t -> p (c n t)"),
+                out=w_codes[:, bank, :, :].rearrange("p c n -> p (c n)").bitcast(FP8X4),
+                scales=w_scales[:, bank, :, :].rearrange("p c n -> p (c n)"),
+                in_=w_grouped[bank][:].rearrange("p c n t -> p (c n t)"),
             )
 
         def mx_group(acc, tile_m, rhs_codes, rhs_scales):
@@ -186,45 +183,57 @@ def tile_gaublock_pb_kernel(
                     out=acc,
                     lhsT=xn_codes[:, pair, c, P * i : P * (i + 1)].bitcast(FP8X4),
                     lhsT_scale=xn_scales[:, pair, c, P * i : P * (i + 1)],
-                    rhs=rhs_codes[c].bitcast(FP8X4),
-                    rhs_scale=rhs_scales[c],
+                    rhs=rhs_codes[:, c, :].bitcast(FP8X4),
+                    rhs_scale=rhs_scales[:, c, :],
                     start=(c == 0),
                     stop=(c == PASSES - 1),
                 )
 
-        def project(chunk, pair):
-            out_sb = result.tile([P, 2, CHUNK], F32, name="out_sb")
+        def multiply(out_sb, chunk, pair, h):
+            bank = CHUNK // BANK * chunk + h
             for i in range(2):
-                for h in range(CHUNK // BANK):
-                    cols = slice(CHUNK * chunk + BANK * h, CHUNK * chunk + BANK * (h + 1))
-                    acc = psum.tile([P, BANK], F32, name="acc", tag="bank")
-                    mx_group(
-                        acc[:],
-                        2 * pair + i,
-                        [w_codes[:, c, cols] for c in range(PASSES)],
-                        [w_scales[:, c, cols] for c in range(PASSES)],
-                    )
-                    nc.vector.tensor_tensor(
-                        out=out_sb[:, i, BANK * h : BANK * (h + 1)], in0=acc[:], in1=bias_all[:, cols], op=ALU.add
-                    )
+                acc = psum.tile([P, BANK], F32, name="acc", tag="bank")
+                mx_group(acc[:], 2 * pair + i, w_codes[:, bank, :, :], w_scales[:, bank, :, :])
+                nc.vector.tensor_tensor(
+                    out=out_sb[:, i, BANK * h : BANK * (h + 1)],
+                    in0=acc[:],
+                    in1=bias_all[:, BANK * bank : BANK * (bank + 1)],
+                    op=ALU.add,
+                )
+
+        def finish(out_sb, chunk, pair):
             nc.scalar.activation(out=out_sb[:], in_=out_sb[:], func=ACT.Silu)
             first = (CHUNK * chunk) % E
             nc.sync.dma_start(
                 out=uv_rows[(CHUNK * chunk) // E][:, 2 * pair : 2 * pair + 2, first : first + CHUNK], in_=out_sb[:]
             )
 
+        def project(chunk, pair):
+            out_sb = result.tile([P, 2, CHUNK], F32, name="out_sb")
+            for h in range(CHUNK // BANK):
+                multiply(out_sb, chunk, pair, h)
+            finish(out_sb, chunk, pair)
+
+        wz_grouped = keep.tile([P, PASSES, S, PACK], BF16, name="wz_grouped", align_bytes=64)
+
+        def group_wz():
+            for c in range(PASSES):
+                regroup(nc.scalar.copy, wz_grouped[:, c, :, :], wz_raw[:, c, :, :])
+
+        def quantise_wz():
+            nc.vector.quantize_mx(
+                out=wz_codes[:].rearrange("p c n -> p (c n)").bitcast(FP8X4),
+                scales=wz_scales[:].rearrange("p c n -> p (c n)"),
+                in_=wz_grouped[:].rearrange("p c n t -> p (c n t)"),
+            )
+
         def project_z():
-            z_sb = result.tile([P, ROW_TILES, S], F32, name="z_sb", tag="out_sb")
+            z_sb = keep.tile([P, ROW_TILES, S], F32, name="z_sb")
             per_bank = BANK // S
             for a in range(ROW_TILES // per_bank):
                 acc = psum.tile([P, per_bank, S], F32, name="acc_z", tag="bank")
                 for i in range(per_bank):
-                    mx_group(
-                        acc[:, i, :],
-                        per_bank * a + i,
-                        [wz_codes[:, c, :] for c in range(PASSES)],
-                        [wz_scales[:, c, :] for c in range(PASSES)],
-                    )
+                    mx_group(acc[:, i, :], per_bank * a + i, wz_codes, wz_scales)
                 nc.vector.tensor_tensor(
                     out=z_sb[:, per_bank * a : per_bank * (a + 1), :],
                     in0=acc[:],
@@ -232,27 +241,81 @@ def tile_gaublock_pb_kernel(
                     op=ALU.add,
                 )
             nc.scalar.activation(out=z_sb[:], in_=z_sb[:], func=ACT.Silu)
+            mapped = []
             for w in range(2):
                 gain = qk_all[:, 2 * w, :].unsqueeze(1).to_broadcast([P, ROW_TILES, S])
                 offset = qk_all[:, 2 * w + 1, :].unsqueeze(1).to_broadcast([P, ROW_TILES, S])
-                mapped = result.tile([P, ROW_TILES, S], F32, name="mapped", tag="out_sb")
-                nc.gpsimd.tensor_tensor(out=mapped[:], in0=z_sb[:], in1=gain, op=ALU.mult)
-                nc.gpsimd.tensor_tensor(out=mapped[:], in0=mapped[:], in1=offset, op=ALU.add)
-                nc.sync.dma_start(out=qk_rows[w], in_=mapped[:])
+                m = keep.tile([P, ROW_TILES, S], F32, name="mapped%d" % w)
+                nc.gpsimd.tensor_tensor(out=m[:], in0=z_sb[:], in1=gain, op=ALU.mult)
+                nc.gpsimd.tensor_tensor(out=m[:], in0=m[:], in1=offset, op=ALU.add)
+                mapped.append(m)
+            return mapped
 
-        layer_norm(0)
+        def store_qk(mapped):
+            for w in range(2):
+                nc.sync.dma_start(out=qk_rows[w], in_=mapped[w][:])
+
+        vec, act = nc.vector.tensor_copy, nc.scalar.copy
+
+        g_cols = keep.tile([P, K_TILES], F32, name="g_cols")
+        b_cols = keep.tile([P, K_TILES], F32, name="b_cols")
+        nc.vector.tensor_copy(out=g_cols[:], in_=g_raw[:].rearrange("p c t -> p (c t)"))
+        nc.vector.tensor_copy(out=b_cols[:], in_=b_raw[:].rearrange("p c t -> p (c t)"))
+        normalise(0)
+        group_w(0, 0, vec)
+        group_w(1, 0, act)
+        normalise(1)
+        turn(0)
+        group_w(0, 1, vec)
+        group_w(1, 1, act)
+        group_x(0)
         quantise_w(0)
-        for pair in range(PAIRS):
-            if pair + 1 < PAIRS:
-                layer_norm(pair + 1)
-            else:
-                quantise_w(1)
-            project(0, pair)
+        quantise_x(0)
+        normalise(2)
+        turn(1)
+        group_w(2, 0, act)
+        out_sb = result.tile([P, 2, CHUNK], F32, name="out_sb")
+        multiply(out_sb, 0, 0, 0)
+        quantise_w(1)
+        multiply(out_sb, 0, 0, 1)
+        finish(out_sb, 0, 0)
+        group_x(1)
+        normalise(3)
+        quantise_x(1)
+        turn(2)
+        group_w(2, 1, act)
+        project(0, 1)
+        group_x(2)
+        quantise_w(2)
+        quantise_x(2)
+        turn(3)
+        group_w(3, 0, act)
+        project(0, 2)
+        group_x(3)
+        group_w(3, 1, vec)
+        quantise_x(3)
+        project(0, 3)
+        quantise_w(3)
+        for c in range(PASSES):
+            load_w(CHUNKS - 1, c)
+
+        mapped = None
         for chunk in range(1, CHUNKS):
-            if chunk + 1 < CHUNKS:
-                quantise_w(chunk + 1)
-            else:
-                quantise_wz()
-                project_z()
+            if chunk == CHUNKS - 1:
+                mapped = project_z()
             for pair in range(PAIRS):
+                bank = CHUNK // BANK * (chunk + 1) + pair // 2
+                if chunk + 1 < CHUNKS and pair % 2 == 0:
+                    group_w(bank, 0, act)
+                    if pair == 2 and chunk + 2 == CHUNKS:
+                        group_wz()
                 project(chunk, pair)
+                if chunk + 1 < CHUNKS:
+                    if pair % 2 == 0:
+                        group_w(bank, 1, vec)
+                    else:
+                        quantise_w(bank)
+                        if pair == 3 and chunk + 2 == CHUNKS:
+                            quantise_wz()
+                if mapped is not None and pair == 2:
+                    store_qk(mapped)

@@ -111,6 +111,8 @@ def tile_gaublock_pb_kernel(
                 nc.vector.bn_aggr(out=mean_var[:, i, :], in_=stats[:, i, :, :].rearrange("p a b -> p (a b)"))
             var_eps = stat.tile([P, 2], F32, name="var_eps")
             nc.gpsimd.tensor_scalar_add(out=var_eps[:], in0=mean_var[:, :, 1], scalar1=LN_EPS)
+            neg_mean = stat.tile([P, 2], F32, name="neg_mean")
+            nc.gpsimd.tensor_scalar_mul(out=neg_mean[:], in0=mean_var[:, :, 0], scalar1=-1.0)
             rstd = stat.tile([P, 2], F32, name="rstd")
             nc.gpsimd.tensor_tensor(out=rstd[:], in0=var_eps[:], in1=minus_half[:], op=ALU.pow)
             for i in range(2):
@@ -118,9 +120,9 @@ def tile_gaublock_pb_kernel(
                 nc.gpsimd.tensor_scalar(
                     out=y[:],
                     in0=x_sb[:, 2 * pair + i, :].rearrange("p (c q t) -> p c t q", c=PASSES, t=PACK),
-                    scalar1=mean_var[:, i, 0:1],
+                    scalar1=neg_mean[:, i : i + 1],
                     scalar2=rstd[:, i : i + 1],
-                    op0=ALU.subtract,
+                    op0=ALU.add,
                     op1=ALU.mult,
                 )
                 y_rows[(pair, i)] = y

@@ -40,13 +40,14 @@ def tile_gaublock_pb_kernel(
 
     with ExitStack() as ctx:
         keep = ctx.enter_context(tc.tile_pool(name="keep", bufs=1))
-        stat = ctx.enter_context(tc.tile_pool(name="stat", bufs=2))
+        stat = ctx.enter_context(tc.tile_pool(name="stat", bufs=4))
         normed = ctx.enter_context(tc.tile_pool(name="normed", bufs=4))
         raw = ctx.enter_context(tc.tile_pool(name="raw", bufs=6))
         stage = ctx.enter_context(tc.tile_pool(name="stage", bufs=2))
         wstage = ctx.enter_context(tc.tile_pool(name="wstage", bufs=3))
-        result = ctx.enter_context(tc.tile_pool(name="result", bufs=4))
-        psum = ctx.enter_context(tc.psum_pool(name="psum", bufs=8))
+        result = ctx.enter_context(tc.tile_pool(name="result", bufs=5))
+        psum = ctx.enter_context(tc.psum_pool(name="psum", bufs=6))
+        moved = ctx.enter_context(tc.psum_pool(name="moved", bufs=2))
         ctx.enter_context(tc.manual_schedule())
 
         g_raw = keep.tile([P, PASSES, PACK], BF16, name="g_raw")
@@ -55,8 +56,12 @@ def tile_gaublock_pb_kernel(
         nc.scalar.dma_start(out=b_raw[:], in_=ln_b.rearrange("(c p t) -> p c t", p=P, t=PACK))
         minus_half = keep.tile([P, 2], F32, name="minus_half")
         nc.vector.memset(minus_half[:], -0.5)
+        warm = keep.tile([P, 1], F32, name="warm")
+        nc.scalar.activation(out=warm[:], in_=minus_half[:, 0:1], func=ACT.Silu)
         ident = keep.tile([P, P], F32, name="ident")
         make_identity(nc, ident[:])
+        ident_bf16 = keep.tile([P, P], BF16, name="ident_bf16")
+        nc.gpsimd.tensor_copy(out=ident_bf16[:], in_=ident[:])
 
         x_sb = keep.tile([P, ROW_TILES, D], BF16, name="x_sb")
         bias_all = keep.tile([P, F], BF16, name="bias_all")
@@ -71,12 +76,20 @@ def tile_gaublock_pb_kernel(
             w_raw[(chunk, c)] = raw.tile([P, PACK, CHUNK], BF16, name="w_raw")
             nc.sync.dma_start(out=w_raw[(chunk, c)][:], in_=w_rows[:, c, :, CHUNK * chunk : CHUNK * (chunk + 1)])
 
+        def load_half(h, c):
+            if h == 0:
+                w_raw[(0, c)] = raw.tile([P, PACK, CHUNK], BF16, name="w_raw")
+            cols = slice(BANK * h, BANK * (h + 1))
+            nc.sync.dma_start(out=w_raw[(0, c)][:, :, cols], in_=w_rows[:, c, :, cols])
+
         load_x(0)
-        load_w(0, 0)
+        load_half(0, 0)
         load_x(1)
-        load_w(0, 1)
+        load_half(0, 1)
         load_x(2)
         load_x(3)
+        load_half(1, 0)
+        load_half(1, 1)
         nc.sync.dma_start(out=bias_all[:], in_=b_in.partition_broadcast(P))
         for chunk in range(1, CHUNKS - 1):
             for c in range(PASSES):
@@ -99,33 +112,44 @@ def tile_gaublock_pb_kernel(
                 in_=src.rearrange("p t (a i) -> p a t i", i=4),
             )
 
-        y_rows, k_tiles, xn_grouped, w_grouped = {}, {}, {}, {}
+        mean_var, rstds, y_rows, k_tiles, xn_grouped, w_grouped = {}, {}, {}, {}, {}, {}
+
+        def measure(m):
+            pair, i = divmod(m, 2)
+            if i == 0:
+                mean_var[pair] = stat.tile([P, 2, 2], F32, name="mean_var")
+            stats = stat.tile([P, 2, 6], F32, name="stats")
+            for h in range(2):
+                nc.vector.bn_stats(out=stats[:, h, :], in_=x_sb[:, m, 512 * h : 512 * (h + 1)])
+            nc.vector.bn_aggr(out=mean_var[pair][:, i, :], in_=stats[:].rearrange("p a b -> p (a b)"))
+
+        def invert(pair):
+            var_eps = stat.tile([P, 2], F32, name="var_eps")
+            nc.vector.tensor_scalar_add(out=var_eps[:], in0=mean_var[pair][:, :, 1], scalar1=LN_EPS)
+            rstds[pair] = stat.tile([P, 2], F32, name="rstd")
+            nc.gpsimd.tensor_tensor(out=rstds[pair][:], in0=var_eps[:], in1=minus_half[:], op=ALU.pow)
 
         def normalise(pair):
-            stats = stat.tile([P, 2, 2, 6], F32, name="stats")
-            mean_var = stat.tile([P, 2, 2], F32, name="mean_var")
-            for i in range(2):
-                for h in range(2):
-                    nc.vector.bn_stats(out=stats[:, i, h, :], in_=x_sb[:, 2 * pair + i, 512 * h : 512 * (h + 1)])
-            for i in range(2):
-                nc.vector.bn_aggr(out=mean_var[:, i, :], in_=stats[:, i, :, :].rearrange("p a b -> p (a b)"))
-            var_eps = stat.tile([P, 2], F32, name="var_eps")
-            nc.gpsimd.tensor_scalar_add(out=var_eps[:], in0=mean_var[:, :, 1], scalar1=LN_EPS)
-            neg_mean = stat.tile([P, 2], F32, name="neg_mean")
-            nc.gpsimd.tensor_scalar_mul(out=neg_mean[:], in0=mean_var[:, :, 0], scalar1=-1.0)
-            rstd = stat.tile([P, 2], F32, name="rstd")
-            nc.gpsimd.tensor_tensor(out=rstd[:], in0=var_eps[:], in1=minus_half[:], op=ALU.pow)
+            means, rstd = mean_var[pair], rstds[pair]
+            shift = stat.tile([P, 1], F32, name="shift")
+            nc.vector.scalar_tensor_tensor(
+                out=shift[:], in0=means[:, 1, 0:1], scalar=-1.0, in1=rstd[:, 1:2], op0=ALU.mult, op1=ALU.mult
+            )
             for i in range(2):
                 y = normed.tile([P, PASSES, PACK, P], F32, name="y")
-                nc.gpsimd.tensor_scalar(
-                    out=y[:],
-                    in0=x_sb[:, 2 * pair + i, :].rearrange("p (c q t) -> p c t q", c=PASSES, t=PACK),
-                    scalar1=neg_mean[:, i : i + 1],
-                    scalar2=rstd[:, i : i + 1],
-                    op0=ALU.add,
-                    op1=ALU.mult,
-                )
                 y_rows[(pair, i)] = y
+                x_k = x_sb[:, 2 * pair + i, :].rearrange("p (c q t) -> p c t q", c=PASSES, t=PACK)
+                if i == 0:
+                    nc.vector.tensor_scalar(
+                        out=y[:],
+                        in0=x_k,
+                        scalar1=means[:, i, 0:1],
+                        scalar2=rstd[:, i : i + 1],
+                        op0=ALU.subtract,
+                        op1=ALU.mult,
+                    )
+                else:
+                    nc.scalar.activation(out=y[:], in_=x_k, func=ACT.Identity, scale=rstd[:, 1:2], bias=shift[:])
 
         def turn(pair):
             k_tiles[pair] = stage.tile([P, K_TILES, 2 * P], BF16, name="k_tiles")
@@ -171,6 +195,47 @@ def tile_gaublock_pb_kernel(
             chunk, h = divmod(bank, CHUNK // BANK)
             regroup(copy, w_grouped[bank][:, c, :, :], w_raw[(chunk, c)][:, :, BANK * h : BANK * (h + 1)])
 
+        in_flight = {}
+
+        def move_w(bank, c):
+            chunk, h = divmod(bank, CHUNK // BANK)
+            for a in range(2):
+                ps = moved.tile([P, 2, P, PACK], BF16, name="ps")
+                in_flight[(bank, c, a)] = ps
+                for b in range(2):
+                    first = BANK * h + P * (2 * a + b)
+                    nc.tensor.matmul(
+                        out=ps[:, b, :, :].rearrange("p n t -> p (n t)"),
+                        lhsT=ident_bf16[:],
+                        rhs=w_raw[(chunk, c)][:, :, first : first + P].rearrange("p t n -> p n t"),
+                        start=True,
+                        stop=True,
+                    )
+
+        def land_w(bank, c):
+            if bank not in w_grouped:
+                w_grouped[bank] = wstage.tile([P, PASSES, BANK, PACK], BF16, name="w_grouped", align_bytes=64)
+            for a in range(2):
+                nc.scalar.copy(
+                    out=w_grouped[bank][:, c, 2 * P * a : 2 * P * (a + 1), :].rearrange("p n t -> p (n t)"),
+                    in_=in_flight[(bank, c, a)][:].rearrange("p b n t -> p (b n t)"),
+                )
+
+        def shift_w(bank, c):
+            if bank not in w_grouped:
+                w_grouped[bank] = wstage.tile([P, PASSES, BANK, PACK], BF16, name="w_grouped", align_bytes=64)
+            chunk, h = divmod(bank, CHUNK // BANK)
+            for a in range(4):
+                first = BANK * h + P * a
+                nc.gpsimd.tensor_scalar(
+                    out=w_grouped[bank][:, c, P * a : P * (a + 1), :],
+                    in0=w_raw[(chunk, c)][:, :, first : first + P].rearrange("p t n -> p n t"),
+                    scalar1=1.0,
+                    scalar2=0.0,
+                    op0=ALU.mult,
+                    op1=ALU.add,
+                )
+
         def quantise_w(bank):
             nc.vector.quantize_mx(
                 out=w_codes[:, bank, :, :].rearrange("p c n -> p (c n)").bitcast(FP8X4),
@@ -191,30 +256,30 @@ def tile_gaublock_pb_kernel(
                     stop=(c == PASSES - 1),
                 )
 
-        def multiply(out_sb, chunk, pair, h):
-            bank = CHUNK // BANK * chunk + h
-            for i in range(2):
+        outs = {}
+
+        def multiply(bank, first, count, tiles=4):
+            key = (bank, first // tiles * tiles, tiles)
+            if key not in outs:
+                outs[key] = result.tile([P, tiles, BANK], F32, name="out_sb")
+            out_sb = outs[key]
+            for i in range(count):
                 acc = psum.tile([P, BANK], F32, name="acc", tag="bank")
-                mx_group(acc[:], 2 * pair + i, w_codes[:, bank, :, :], w_scales[:, bank, :, :])
+                mx_group(acc[:], first + i, w_codes[:, bank, :, :], w_scales[:, bank, :, :])
                 nc.vector.tensor_tensor(
-                    out=out_sb[:, i, BANK * h : BANK * (h + 1)],
-                    in0=acc[:],
-                    in1=bias_all[:, BANK * bank : BANK * (bank + 1)],
-                    op=ALU.add,
+                    out=out_sb[:, (first + i) % tiles, :], in0=acc[:], in1=bias_all[:, BANK * bank : BANK * (bank + 1)], op=ALU.add
                 )
 
-        def finish(out_sb, chunk, pair):
-            nc.scalar.activation(out=out_sb[:], in_=out_sb[:], func=ACT.Silu)
-            first = (CHUNK * chunk) % E
-            nc.sync.dma_start(
-                out=uv_rows[(CHUNK * chunk) // E][:, 2 * pair : 2 * pair + 2, first : first + CHUNK], in_=out_sb[:]
-            )
-
-        def project(chunk, pair):
-            out_sb = result.tile([P, 2, CHUNK], F32, name="out_sb")
-            for h in range(CHUNK // BANK):
-                multiply(out_sb, chunk, pair, h)
-            finish(out_sb, chunk, pair)
+        def finish(bank, first, count, pieces=1):
+            out_sb = outs[(bank, first, count)]
+            col = (BANK * bank) % E
+            step = count // pieces
+            for a in range(0, count, step):
+                part = out_sb[:, a : a + step, :]
+                nc.scalar.activation(out=part, in_=part, func=ACT.Silu)
+                nc.sync.dma_start(
+                    out=uv_rows[(BANK * bank) // E][:, first + a : first + a + step, col : col + BANK], in_=part
+                )
 
         wz_grouped = keep.tile([P, PASSES, S, PACK], BF16, name="wz_grouped", align_bytes=64)
 
@@ -257,67 +322,92 @@ def tile_gaublock_pb_kernel(
             for w in range(2):
                 nc.sync.dma_start(out=qk_rows[w], in_=mapped[w][:])
 
-        vec, act = nc.vector.tensor_copy, nc.scalar.copy
-
         g_cols = keep.tile([P, K_TILES], F32, name="g_cols")
         b_cols = keep.tile([P, K_TILES], F32, name="b_cols")
+        banks = 2 * E // BANK
+
+        measure(0)
+        measure(1)
+        invert(0)
+        move_w(0, 0)
+        land_w(0, 0)
+        move_w(0, 1)
+        measure(2)
+        land_w(0, 1)
+        normalise(0)
         nc.vector.tensor_copy(out=g_cols[:], in_=g_raw[:].rearrange("p c t -> p (c t)"))
         nc.vector.tensor_copy(out=b_cols[:], in_=b_raw[:].rearrange("p c t -> p (c t)"))
-        normalise(0)
-        group_w(0, 0, vec)
-        group_w(1, 0, act)
-        normalise(1)
+        measure(3)
+        invert(1)
         turn(0)
-        group_w(0, 1, vec)
-        group_w(1, 1, act)
-        group_x(0)
+        measure(4)
+        normalise(1)
         quantise_w(0)
-        quantise_x(0)
-        normalise(2)
         turn(1)
-        group_w(2, 0, act)
-        out_sb = result.tile([P, 2, CHUNK], F32, name="out_sb")
-        multiply(out_sb, 0, 0, 0)
-        quantise_w(1)
-        multiply(out_sb, 0, 0, 1)
-        finish(out_sb, 0, 0)
+        measure(5)
+        invert(2)
+        group_x(0)
+        measure(6)
+        move_w(1, 0)
+        land_w(1, 0)
+        normalise(2)
+        quantise_x(0)
+        turn(2)
+        measure(7)
+        invert(3)
         group_x(1)
+        move_w(1, 1)
+        land_w(1, 1)
+        multiply(0, 0, 2, 2)
         normalise(3)
         quantise_x(1)
-        turn(2)
-        group_w(2, 1, act)
-        project(0, 1)
-        group_x(2)
-        quantise_w(2)
-        quantise_x(2)
         turn(3)
-        group_w(3, 0, act)
-        project(0, 2)
+        move_w(2, 0)
+        group_x(2)
+        multiply(0, 2, 2, 2)
+        finish(0, 0, 2)
+        quantise_x(2)
+        quantise_w(1)
+        land_w(2, 0)
         group_x(3)
-        group_w(3, 1, vec)
+        move_w(2, 1)
+        multiply(0, 4, 2, 2)
+        finish(0, 2, 2)
         quantise_x(3)
-        project(0, 3)
-        quantise_w(3)
-        for c in range(PASSES):
-            load_w(CHUNKS - 1, c)
-
-        mapped = None
-        for chunk in range(1, CHUNKS):
-            if chunk == CHUNKS - 1:
+        land_w(2, 1)
+        move_w(3, 0)
+        multiply(0, 6, 2, 2)
+        finish(0, 4, 2)
+        multiply(1, 0, 4)
+        finish(0, 6, 2)
+        land_w(3, 0)
+        quantise_w(2)
+        move_w(3, 1)
+        multiply(1, 4, 4)
+        land_w(3, 1)
+        finish(1, 0, 4)
+        load_w(3, 0)
+        load_w(3, 1)
+        last = (1, 4, 4)
+        for bank in range(2, 8):
+            if bank == 5:
+                quantise_wz()
+            if bank == 6:
                 mapped = project_z()
-            for pair in range(PAIRS):
-                bank = CHUNK // BANK * (chunk + 1) + pair // 2
-                if chunk + 1 < CHUNKS and pair % 2 == 0:
-                    group_w(bank, 0, act)
-                    if pair == 2 and chunk + 2 == CHUNKS:
-                        group_wz()
-                project(chunk, pair)
-                if chunk + 1 < CHUNKS:
-                    if pair % 2 == 0:
-                        group_w(bank, 1, vec)
+            for half in range(2):
+                multiply(bank, 4 * half, 2)
+                if half == 1 and bank < 7:
+                    quantise_w(bank + 1)
+                multiply(bank, 4 * half + 2, 2)
+                if bank + 2 < 8:
+                    if half == 0:
+                        move_w(bank + 2, 0)
+                        land_w(bank + 2, 0)
                     else:
-                        quantise_w(bank)
-                        if pair == 3 and chunk + 2 == CHUNKS:
-                            quantise_wz()
-                if mapped is not None and pair == 2:
-                    store_qk(mapped)
+                        shift_w(bank + 2, 1)
+                finish(*last)
+                last = (bank, 4 * half, 4)
+                if bank == 4 and half == 0:
+                    group_wz()
+        finish(*last, pieces=2)
+        store_qk(mapped)

@@ -46,9 +46,7 @@ def tile_gaublock_pb_kernel(
         stage = ctx.enter_context(tc.tile_pool(name="stage", bufs=2))
         wstage = ctx.enter_context(tc.tile_pool(name="wstage", bufs=3))
         result = ctx.enter_context(tc.tile_pool(name="result", bufs=5))
-        psum = ctx.enter_context(tc.psum_pool(name="psum", bufs=6))
-        moved = ctx.enter_context(tc.psum_pool(name="moved", bufs=2))
-        ctx.enter_context(tc.manual_schedule())
+        psum = ctx.enter_context(tc.psum_pool(name="psum", bufs=8))
 
         g_raw = keep.tile([P, PASSES, PACK], BF16, name="g_raw")
         b_raw = keep.tile([P, PASSES, PACK], BF16, name="b_raw")
@@ -60,8 +58,6 @@ def tile_gaublock_pb_kernel(
         nc.scalar.activation(out=warm[:], in_=minus_half[:, 0:1], func=ACT.Silu)
         ident = keep.tile([P, P], F32, name="ident")
         make_identity(nc, ident[:])
-        ident_bf16 = keep.tile([P, P], BF16, name="ident_bf16")
-        nc.gpsimd.tensor_copy(out=ident_bf16[:], in_=ident[:])
 
         x_sb = keep.tile([P, ROW_TILES, D], BF16, name="x_sb")
         bias_all = keep.tile([P, F], BF16, name="bias_all")
@@ -195,32 +191,6 @@ def tile_gaublock_pb_kernel(
             chunk, h = divmod(bank, CHUNK // BANK)
             regroup(copy, w_grouped[bank][:, c, :, :], w_raw[(chunk, c)][:, :, BANK * h : BANK * (h + 1)])
 
-        in_flight = {}
-
-        def move_w(bank, c):
-            chunk, h = divmod(bank, CHUNK // BANK)
-            for a in range(2):
-                ps = moved.tile([P, 2, P, PACK], BF16, name="ps")
-                in_flight[(bank, c, a)] = ps
-                for b in range(2):
-                    first = BANK * h + P * (2 * a + b)
-                    nc.tensor.matmul(
-                        out=ps[:, b, :, :].rearrange("p n t -> p (n t)"),
-                        lhsT=ident_bf16[:],
-                        rhs=w_raw[(chunk, c)][:, :, first : first + P].rearrange("p t n -> p n t"),
-                        start=True,
-                        stop=True,
-                    )
-
-        def land_w(bank, c):
-            if bank not in w_grouped:
-                w_grouped[bank] = wstage.tile([P, PASSES, BANK, PACK], BF16, name="w_grouped", align_bytes=64)
-            for a in range(2):
-                nc.scalar.copy(
-                    out=w_grouped[bank][:, c, 2 * P * a : 2 * P * (a + 1), :].rearrange("p n t -> p (n t)"),
-                    in_=in_flight[(bank, c, a)][:].rearrange("p b n t -> p (b n t)"),
-                )
-
         def shift_w(bank, c):
             if bank not in w_grouped:
                 w_grouped[bank] = wstage.tile([P, PASSES, BANK, PACK], BF16, name="w_grouped", align_bytes=64)
@@ -326,66 +296,61 @@ def tile_gaublock_pb_kernel(
         b_cols = keep.tile([P, K_TILES], F32, name="b_cols")
         banks = 2 * E // BANK
 
+        vcopy, scopy = nc.vector.tensor_copy, nc.scalar.copy
         measure(0)
         measure(1)
         invert(0)
-        move_w(0, 0)
-        land_w(0, 0)
-        move_w(0, 1)
+        group_w(0, 0, scopy)
         measure(2)
-        land_w(0, 1)
         normalise(0)
         nc.vector.tensor_copy(out=g_cols[:], in_=g_raw[:].rearrange("p c t -> p (c t)"))
         nc.vector.tensor_copy(out=b_cols[:], in_=b_raw[:].rearrange("p c t -> p (c t)"))
+        group_w(0, 1, vcopy)
+        turn(0)
         measure(3)
         invert(1)
-        turn(0)
+        quantise_w(0)
         measure(4)
         normalise(1)
-        quantise_w(0)
         turn(1)
-        measure(5)
-        invert(2)
         group_x(0)
-        measure(6)
-        move_w(1, 0)
-        land_w(1, 0)
-        normalise(2)
+        measure(5)
         quantise_x(0)
+        invert(2)
+        group_w(1, 0, scopy)
+        measure(6)
+        multiply(0, 0, 2, 2)
+        normalise(2)
         turn(2)
+        group_x(1)
         measure(7)
         invert(3)
-        group_x(1)
-        move_w(1, 1)
-        land_w(1, 1)
-        multiply(0, 0, 2, 2)
-        normalise(3)
         quantise_x(1)
-        turn(3)
-        move_w(2, 0)
-        group_x(2)
+        group_w(1, 1, vcopy)
         multiply(0, 2, 2, 2)
+        normalise(3)
+        turn(3)
         finish(0, 0, 2)
-        quantise_x(2)
+        group_x(2)
         quantise_w(1)
-        land_w(2, 0)
-        group_x(3)
-        move_w(2, 1)
+        quantise_x(2)
+        group_w(2, 0, scopy)
         multiply(0, 4, 2, 2)
         finish(0, 2, 2)
+        group_x(3)
+        shift_w(2, 1)
+        multiply(1, 0, 2)
         quantise_x(3)
-        land_w(2, 1)
-        move_w(3, 0)
-        multiply(0, 6, 2, 2)
+        multiply(1, 2, 2)
         finish(0, 4, 2)
-        multiply(1, 0, 4)
-        finish(0, 6, 2)
-        land_w(3, 0)
-        quantise_w(2)
-        move_w(3, 1)
-        multiply(1, 4, 4)
-        land_w(3, 1)
+        group_w(3, 0, scopy)
+        multiply(0, 6, 2, 2)
         finish(1, 0, 4)
+        multiply(1, 4, 2)
+        quantise_w(2)
+        finish(0, 6, 2)
+        shift_w(3, 1)
+        multiply(1, 6, 2)
         load_w(3, 0)
         load_w(3, 1)
         last = (1, 4, 4)
@@ -401,8 +366,7 @@ def tile_gaublock_pb_kernel(
                 multiply(bank, 4 * half + 2, 2)
                 if bank + 2 < 8:
                     if half == 0:
-                        move_w(bank + 2, 0)
-                        land_w(bank + 2, 0)
+                        group_w(bank + 2, 0, scopy)
                     else:
                         shift_w(bank + 2, 1)
                 finish(*last)

@@ -42,7 +42,7 @@ def tile_gaublock_pb_kernel(
         keep = ctx.enter_context(tc.tile_pool(name="keep", bufs=1))
         stat = ctx.enter_context(tc.tile_pool(name="stat", bufs=4))
         normed = ctx.enter_context(tc.tile_pool(name="normed", bufs=4))
-        raw = ctx.enter_context(tc.tile_pool(name="raw", bufs=6))
+        raw = ctx.enter_context(tc.tile_pool(name="raw", bufs=4))
         stage = ctx.enter_context(tc.tile_pool(name="stage", bufs=2))
         wstage = ctx.enter_context(tc.tile_pool(name="wstage", bufs=3))
         result = ctx.enter_context(tc.tile_pool(name="result", bufs=5))
@@ -63,7 +63,7 @@ def tile_gaublock_pb_kernel(
         bias_all = keep.tile([P, F], BF16, name="bias_all")
         qk_all = keep.tile([P, 4, S], BF16, name="qk_all")
         wz_raw = keep.tile([P, PASSES, PACK, S], BF16, name="wz_raw")
-        w_raw = {}
+        w_raw, w_half = {}, {}
 
         def load_x(pair):
             nc.sync.dma_start(out=x_sb[:, 2 * pair : 2 * pair + 2, :], in_=x_rows[:, 2 * pair : 2 * pair + 2, :])
@@ -73,10 +73,14 @@ def tile_gaublock_pb_kernel(
             nc.sync.dma_start(out=w_raw[(chunk, c)][:], in_=w_rows[:, c, :, CHUNK * chunk : CHUNK * (chunk + 1)])
 
         def load_half(h, c):
-            if h == 0:
-                w_raw[(0, c)] = raw.tile([P, PACK, CHUNK], BF16, name="w_raw")
-            cols = slice(BANK * h, BANK * (h + 1))
-            nc.sync.dma_start(out=w_raw[(0, c)][:, :, cols], in_=w_rows[:, c, :, cols])
+            w_half[(h, c)] = keep.tile([P, PACK, BANK], BF16, name="w_half%d_%d" % (h, c))
+            nc.sync.dma_start(out=w_half[(h, c)][:], in_=w_rows[:, c, :, BANK * h : BANK * (h + 1)])
+
+        def columns(bank, c):
+            chunk, h = divmod(bank, CHUNK // BANK)
+            if chunk == 0:
+                return w_half[(h, c)][:]
+            return w_raw[(chunk, c)][:, :, BANK * h : BANK * (h + 1)]
 
         load_x(0)
         load_half(0, 0)
@@ -188,18 +192,15 @@ def tile_gaublock_pb_kernel(
         def group_w(bank, c, copy):
             if bank not in w_grouped:
                 w_grouped[bank] = wstage.tile([P, PASSES, BANK, PACK], BF16, name="w_grouped", align_bytes=64)
-            chunk, h = divmod(bank, CHUNK // BANK)
-            regroup(copy, w_grouped[bank][:, c, :, :], w_raw[(chunk, c)][:, :, BANK * h : BANK * (h + 1)])
+            regroup(copy, w_grouped[bank][:, c, :, :], columns(bank, c))
 
         def shift_w(bank, c):
             if bank not in w_grouped:
                 w_grouped[bank] = wstage.tile([P, PASSES, BANK, PACK], BF16, name="w_grouped", align_bytes=64)
-            chunk, h = divmod(bank, CHUNK // BANK)
             for a in range(4):
-                first = BANK * h + P * a
                 nc.gpsimd.tensor_scalar(
                     out=w_grouped[bank][:, c, P * a : P * (a + 1), :],
-                    in0=w_raw[(chunk, c)][:, :, first : first + P].rearrange("p t n -> p n t"),
+                    in0=columns(bank, c)[:, :, P * a : P * (a + 1)].rearrange("p t n -> p n t"),
                     scalar1=1.0,
                     scalar2=0.0,
                     op0=ALU.mult,
@@ -278,34 +279,28 @@ def tile_gaublock_pb_kernel(
                     op=ALU.add,
                 )
             nc.scalar.activation(out=z_sb[:], in_=z_sb[:], func=ACT.Silu)
-            mapped = []
             for w in range(2):
                 gain = qk_all[:, 2 * w, :].unsqueeze(1).to_broadcast([P, ROW_TILES, S])
                 offset = qk_all[:, 2 * w + 1, :].unsqueeze(1).to_broadcast([P, ROW_TILES, S])
                 m = keep.tile([P, ROW_TILES, S], F32, name="mapped%d" % w)
                 nc.gpsimd.tensor_tensor(out=m[:], in0=z_sb[:], in1=gain, op=ALU.mult)
                 nc.gpsimd.tensor_tensor(out=m[:], in0=m[:], in1=offset, op=ALU.add)
-                mapped.append(m)
-            return mapped
-
-        def store_qk(mapped):
-            for w in range(2):
-                nc.sync.dma_start(out=qk_rows[w], in_=mapped[w][:])
+                nc.gpsimd.dma_start(out=qk_rows[w], in_=m[:])
 
         g_cols = keep.tile([P, K_TILES], F32, name="g_cols")
         b_cols = keep.tile([P, K_TILES], F32, name="b_cols")
         banks = 2 * E // BANK
 
-        vcopy, scopy = nc.vector.tensor_copy, nc.scalar.copy
+        scopy = nc.scalar.copy
         measure(0)
         measure(1)
         invert(0)
         group_w(0, 0, scopy)
+        group_w(0, 1, scopy)
         measure(2)
         normalise(0)
-        nc.vector.tensor_copy(out=g_cols[:], in_=g_raw[:].rearrange("p c t -> p (c t)"))
-        nc.vector.tensor_copy(out=b_cols[:], in_=b_raw[:].rearrange("p c t -> p (c t)"))
-        group_w(0, 1, vcopy)
+        nc.gpsimd.tensor_copy(out=g_cols[:], in_=g_raw[:].rearrange("p c t -> p (c t)"))
+        nc.gpsimd.tensor_copy(out=b_cols[:], in_=b_raw[:].rearrange("p c t -> p (c t)"))
         turn(0)
         measure(3)
         invert(1)
@@ -326,7 +321,7 @@ def tile_gaublock_pb_kernel(
         measure(7)
         invert(3)
         quantise_x(1)
-        group_w(1, 1, vcopy)
+        shift_w(1, 1)
         multiply(0, 2, 2, 2)
         normalise(3)
         turn(3)
@@ -355,23 +350,24 @@ def tile_gaublock_pb_kernel(
         load_w(3, 1)
         last = (1, 4, 4)
         for bank in range(2, 8):
-            if bank == 5:
+            if bank == 4:
                 quantise_wz()
-            if bank == 6:
-                mapped = project_z()
+            if bank == 5:
+                project_z()
             for half in range(2):
                 multiply(bank, 4 * half, 2)
                 if half == 1 and bank < 7:
                     quantise_w(bank + 1)
                 multiply(bank, 4 * half + 2, 2)
                 if bank + 2 < 8:
-                    if half == 0:
+                    if half == 0 and bank % 2 == 0:
                         group_w(bank + 2, 0, scopy)
+                    elif half == 0:
+                        shift_w(bank + 2, 0)
                     else:
                         shift_w(bank + 2, 1)
                 finish(*last)
                 last = (bank, 4 * half, 4)
-                if bank == 4 and half == 0:
+                if bank == 3 and half == 0:
                     group_wz()
         finish(*last, pieces=2)
-        store_qk(mapped)

@@ -41,12 +41,14 @@ def tile_gaublock_pb_kernel(
     with ExitStack() as ctx:
         keep = ctx.enter_context(tc.tile_pool(name="keep", bufs=1))
         stat = ctx.enter_context(tc.tile_pool(name="stat", bufs=4))
-        normed = ctx.enter_context(tc.tile_pool(name="normed", bufs=4))
-        raw = ctx.enter_context(tc.tile_pool(name="raw", bufs=4))
+        normed = ctx.enter_context(tc.tile_pool(name="normed", bufs=5))
+        raw = ctx.enter_context(tc.tile_pool(name="raw", bufs=5))
         stage = ctx.enter_context(tc.tile_pool(name="stage", bufs=2))
         wstage = ctx.enter_context(tc.tile_pool(name="wstage", bufs=3))
         result = ctx.enter_context(tc.tile_pool(name="result", bufs=5))
         psum = ctx.enter_context(tc.psum_pool(name="psum", bufs=8))
+
+        ctx.enter_context(tc.manual_schedule())
 
         g_raw = keep.tile([P, PASSES, PACK], BF16, name="g_raw")
         b_raw = keep.tile([P, PASSES, PACK], BF16, name="b_raw")
@@ -58,10 +60,11 @@ def tile_gaublock_pb_kernel(
         nc.scalar.activation(out=warm[:], in_=minus_half[:, 0:1], func=ACT.Silu)
         ident = keep.tile([P, P], F32, name="ident")
         make_identity(nc, ident[:])
+        ident_bf16 = keep.tile([P, P], BF16, name="ident_bf16")
+        nc.gpsimd.tensor_copy(out=ident_bf16[:], in_=ident[:])
 
         x_sb = keep.tile([P, ROW_TILES, D], BF16, name="x_sb")
-        bias_all = keep.tile([P, F], BF16, name="bias_all")
-        qk_all = keep.tile([P, 4, S], BF16, name="qk_all")
+        bias_all = keep.tile([P, E + E], BF16, name="bias_all")
         wz_raw = keep.tile([P, PASSES, PACK, S], BF16, name="wz_raw")
         w_raw, w_half = {}, {}
 
@@ -82,7 +85,8 @@ def tile_gaublock_pb_kernel(
                 return w_half[(h, c)][:]
             return w_raw[(chunk, c)][:, :, BANK * h : BANK * (h + 1)]
 
-        load_x(0)
+        for m in range(2):
+            nc.sync.dma_start(out=x_sb[:, m : m + 1, :], in_=x_rows[:, m : m + 1, :])
         load_half(0, 0)
         load_x(1)
         load_half(0, 1)
@@ -90,14 +94,18 @@ def tile_gaublock_pb_kernel(
         load_x(3)
         load_half(1, 0)
         load_half(1, 1)
-        nc.sync.dma_start(out=bias_all[:], in_=b_in.partition_broadcast(P))
+        nc.sync.dma_start(out=bias_all[:], in_=b_in[0 : E + E].partition_broadcast(P))
         for chunk in range(1, CHUNKS - 1):
             for c in range(PASSES):
                 load_w(chunk, c)
+        load_w(CHUNKS - 1, 1)
         for c in range(PASSES):
             nc.sync.dma_start(out=wz_raw[:, c, :, :], in_=w_rows[:, c, :, 2 * E : F])
-        for i, vec in enumerate((gamma_q, beta_q, gamma_k, beta_k)):
-            nc.sync.dma_start(out=qk_all[:, i, :], in_=vec.partition_broadcast(P))
+        z_rows = keep.tile([P, S], BF16, name="z_rows")
+        nc.gpsimd.memset(z_rows[:], 0.0)
+        for i, vec in enumerate((b_in[E + E : F], gamma_q, beta_q, gamma_k, beta_k)):
+            nc.sync.dma_start(out=z_rows[i : i + 1, :], in_=vec.unsqueeze(0))
+        z_cols = keep.tile([P, 8], F32, name="z_cols")
 
         xn_codes = keep.tile([P, PAIRS, PASSES, 2 * P], U32, name="xn_codes", align_bytes=64)
         xn_scales = keep.tile([P, PAIRS, PASSES, 2 * P], U8, name="xn_scales", align_bytes=64)
@@ -112,16 +120,20 @@ def tile_gaublock_pb_kernel(
                 in_=src.rearrange("p t (a i) -> p a t i", i=4),
             )
 
-        mean_var, rstds, y_rows, k_tiles, xn_grouped, w_grouped = {}, {}, {}, {}, {}, {}
+        half_stats, mean_var, rstds, y_rows, k_tiles, xn_grouped, w_grouped = {}, {}, {}, {}, {}, {}, {}
 
         def measure(m):
             pair, i = divmod(m, 2)
             if i == 0:
                 mean_var[pair] = stat.tile([P, 2, 2], F32, name="mean_var")
             stats = stat.tile([P, 2, 6], F32, name="stats")
+            half_stats[m] = stats
             for h in range(2):
                 nc.vector.bn_stats(out=stats[:, h, :], in_=x_sb[:, m, 512 * h : 512 * (h + 1)])
-            nc.vector.bn_aggr(out=mean_var[pair][:, i, :], in_=stats[:].rearrange("p a b -> p (a b)"))
+
+        def merge(m):
+            pair, i = divmod(m, 2)
+            nc.vector.bn_aggr(out=mean_var[pair][:, i, :], in_=half_stats[m][:].rearrange("p a b -> p (a b)"))
 
         def invert(pair):
             var_eps = stat.tile([P, 2], F32, name="var_eps")
@@ -229,28 +241,41 @@ def tile_gaublock_pb_kernel(
 
         outs = {}
 
+        def add_bias(out, tile_m, bank):
+            acc = psum.tile([P, BANK], F32, name="acc", tag="bank")
+            mx_group(acc[:], tile_m, w_codes[:, bank, :, :], w_scales[:, bank, :, :])
+            nc.vector.tensor_tensor(out=out, in0=acc[:], in1=bias_all[:, BANK * bank : BANK * (bank + 1)], op=ALU.add)
+
         def multiply(bank, first, count, tiles=4):
             key = (bank, first // tiles * tiles, tiles)
             if key not in outs:
                 outs[key] = result.tile([P, tiles, BANK], F32, name="out_sb")
-            out_sb = outs[key]
             for i in range(count):
-                acc = psum.tile([P, BANK], F32, name="acc", tag="bank")
-                mx_group(acc[:], first + i, w_codes[:, bank, :, :], w_scales[:, bank, :, :])
-                nc.vector.tensor_tensor(
-                    out=out_sb[:, (first + i) % tiles, :], in0=acc[:], in1=bias_all[:, BANK * bank : BANK * (bank + 1)], op=ALU.add
-                )
+                add_bias(outs[key][:, (first + i) % tiles, :], first + i, bank)
 
-        def finish(bank, first, count, pieces=1):
+        def finish(bank, first, count):
             out_sb = outs[(bank, first, count)]
             col = (BANK * bank) % E
-            step = count // pieces
-            for a in range(0, count, step):
-                part = out_sb[:, a : a + step, :]
+            nc.scalar.activation(out=out_sb[:], in_=out_sb[:], func=ACT.Silu)
+            nc.sync.dma_start(
+                out=uv_rows[(BANK * bank) // E][:, first : first + count, col : col + BANK], in_=out_sb[:]
+            )
+
+        def project(chunk, pair):
+            out_sb = result.tile([P, 2, CHUNK], F32, name="out_sb")
+            outs[(chunk, pair)] = out_sb
+            halves = range(CHUNK // BANK)
+            order = [(i, h) for i in range(2) for h in halves] if chunk == CHUNKS - 1 else [(i, h) for h in halves for i in range(2)]
+            for i, h in order:
+                add_bias(out_sb[:, i, BANK * h : BANK * (h + 1)], 2 * pair + i, CHUNK // BANK * chunk + h)
+
+        def conclude(chunk, pair, first, count, width=CHUNK):
+            for col in range(0, CHUNK, width):
+                part = outs[(chunk, pair)][:, first : first + count, col : col + width]
                 nc.scalar.activation(out=part, in_=part, func=ACT.Silu)
-                nc.sync.dma_start(
-                    out=uv_rows[(BANK * bank) // E][:, first + a : first + a + step, col : col + BANK], in_=part
-                )
+                base = (CHUNK * chunk) % E + col
+                rows = slice(2 * pair + first, 2 * pair + first + count)
+                nc.sync.dma_start(out=uv_rows[(CHUNK * chunk) // E][:, rows, base : base + width], in_=part)
 
         wz_grouped = keep.tile([P, PASSES, S, PACK], BF16, name="wz_grouped", align_bytes=64)
 
@@ -265,109 +290,162 @@ def tile_gaublock_pb_kernel(
                 in_=wz_grouped[:].rearrange("p c n t -> p (c n t)"),
             )
 
+        z_tiles = {}
+
+        def turn_vectors():
+            cols = psum.tile([P, S], F32, name="z_turned", tag="bank")
+            nc.tensor.matmul(out=cols[:], lhsT=z_rows[:], rhs=ident_bf16[:], start=True, stop=True)
+            nc.scalar.copy(out=z_cols[:], in_=cols[:, 0:8])
+
         def project_z():
-            z_sb = keep.tile([P, ROW_TILES, S], F32, name="z_sb")
-            per_bank = BANK // S
-            for a in range(ROW_TILES // per_bank):
-                acc = psum.tile([P, per_bank, S], F32, name="acc_z", tag="bank")
-                for i in range(per_bank):
-                    mx_group(acc[:, i, :], per_bank * a + i, wz_codes, wz_scales)
-                nc.vector.tensor_tensor(
-                    out=z_sb[:, per_bank * a : per_bank * (a + 1), :],
-                    in0=acc[:],
-                    in1=bias_all[:, 2 * E : F].unsqueeze(1).to_broadcast([P, per_bank, S]),
-                    op=ALU.add,
+            z_t = normed.tile([P, ROWS], F32, name="z_t", tag="y")
+            z_tiles["z"] = z_t
+            for a in range(2):
+                acc = psum.tile([P, 2, 2 * P], F32, name="acc_z", tag="bank")
+                for b in range(2):
+                    for c in range(PASSES):
+                        nc.tensor.matmul_mx(
+                            out=acc[:, b, :],
+                            lhsT=wz_codes[:, c, :].bitcast(FP8X4),
+                            lhsT_scale=wz_scales[:, c, :],
+                            rhs=xn_codes[:, 2 * a + b, c, :].bitcast(FP8X4),
+                            rhs_scale=xn_scales[:, 2 * a + b, c, :],
+                            start=(c == 0),
+                            stop=(c == PASSES - 1),
+                        )
+                nc.scalar.activation(
+                    out=z_t[:, BANK * a : BANK * (a + 1)],
+                    in_=acc[:].rearrange("p b r -> p (b r)"),
+                    func=ACT.Silu,
+                    bias=z_cols[:, 0:1],
                 )
-            nc.scalar.activation(out=z_sb[:], in_=z_sb[:], func=ACT.Silu)
-            for w in range(2):
-                gain = qk_all[:, 2 * w, :].unsqueeze(1).to_broadcast([P, ROW_TILES, S])
-                offset = qk_all[:, 2 * w + 1, :].unsqueeze(1).to_broadcast([P, ROW_TILES, S])
-                m = keep.tile([P, ROW_TILES, S], F32, name="mapped%d" % w)
-                nc.gpsimd.tensor_tensor(out=m[:], in0=z_sb[:], in1=gain, op=ALU.mult)
-                nc.gpsimd.tensor_tensor(out=m[:], in0=m[:], in1=offset, op=ALU.add)
-                nc.gpsimd.dma_start(out=qk_rows[w], in_=m[:])
+
+        def map_z(w):
+            z_tiles[w] = normed.tile([P, ROWS], F32, name="m_t", tag="y")
+            nc.vector.tensor_scalar(
+                out=z_tiles[w][:],
+                in0=z_tiles["z"][:],
+                scalar1=z_cols[:, 2 * w + 1 : 2 * w + 2],
+                scalar2=z_cols[:, 2 * w + 2 : 2 * w + 3],
+                op0=ALU.mult,
+                op1=ALU.add,
+            )
+
+        def turn_z(w):
+            rows = normed.tile([P, ROW_TILES, S], F32, name="rows", tag="y")
+            for a in range(2):
+                turned = psum.tile([P, 4, S], F32, name="turned_z", tag="bank")
+                for b in range(4):
+                    m = 4 * a + b
+                    nc.tensor.transpose(
+                        out=turned[:, b, :], in_=z_tiles[w][:, P * m : P * (m + 1)], identity=ident[:]
+                    )
+                nc.scalar.copy(out=rows[:, 4 * a : 4 * (a + 1), :], in_=turned[:])
+            nc.sync.dma_start(out=qk_rows[w], in_=rows[:])
 
         g_cols = keep.tile([P, K_TILES], F32, name="g_cols")
         b_cols = keep.tile([P, K_TILES], F32, name="b_cols")
         banks = 2 * E // BANK
 
-        scopy = nc.scalar.copy
+        vcopy, scopy = nc.vector.tensor_copy, nc.scalar.copy
         measure(0)
         measure(1)
-        invert(0)
-        group_w(0, 0, scopy)
-        group_w(0, 1, scopy)
-        measure(2)
-        normalise(0)
+        merge(0)
+        merge(1)
         nc.gpsimd.tensor_copy(out=g_cols[:], in_=g_raw[:].rearrange("p c t -> p (c t)"))
         nc.gpsimd.tensor_copy(out=b_cols[:], in_=b_raw[:].rearrange("p c t -> p (c t)"))
-        turn(0)
+        group_w(0, 0, scopy)
+        measure(2)
+        invert(0)
+        normalise(0)
         measure(3)
+        merge(2)
+        merge(3)
+        group_w(0, 1, scopy)
+        turn(0)
+        measure(4)
         invert(1)
         quantise_w(0)
-        measure(4)
-        normalise(1)
-        turn(1)
-        group_x(0)
         measure(5)
-        quantise_x(0)
-        invert(2)
-        group_w(1, 0, scopy)
+        normalise(1)
+        merge(4)
+        merge(5)
+        group_x(0)
         measure(6)
-        multiply(0, 0, 2, 2)
-        normalise(2)
-        turn(2)
-        group_x(1)
+        invert(2)
+        quantise_x(0)
+        group_w(1, 0, scopy)
+        turn(1)
         measure(7)
+        merge(6)
+        normalise(2)
+        merge(7)
         invert(3)
+        multiply(0, 0, 2, 2)
+        group_x(1)
+        group_w(1, 1, vcopy)
         quantise_x(1)
-        shift_w(1, 1)
-        multiply(0, 2, 2, 2)
-        normalise(3)
-        turn(3)
         finish(0, 0, 2)
+        turn(2)
+        normalise(3)
+        multiply(0, 2, 2, 2)
         group_x(2)
         quantise_w(1)
-        quantise_x(2)
         group_w(2, 0, scopy)
-        multiply(0, 4, 2, 2)
+        turn(3)
+        quantise_x(2)
+        group_w(3, 1, vcopy)
         finish(0, 2, 2)
-        group_x(3)
-        shift_w(2, 1)
-        multiply(1, 0, 2)
-        quantise_x(3)
-        multiply(1, 2, 2)
+        multiply(0, 4, 2, 2)
+        multiply(1, 0, 4)
+        group_w(2, 1, scopy)
         finish(0, 4, 2)
-        group_w(3, 0, scopy)
-        multiply(0, 6, 2, 2)
-        finish(1, 0, 4)
+        group_x(3)
+        shift_w(4, 1)
         multiply(1, 4, 2)
+        quantise_x(3)
         quantise_w(2)
-        finish(0, 6, 2)
-        shift_w(3, 1)
+        group_w(3, 0, scopy)
+        finish(1, 0, 4)
+        shift_w(4, 0)
+        multiply(0, 6, 2, 2)
         multiply(1, 6, 2)
-        load_w(3, 0)
-        load_w(3, 1)
-        last = (1, 4, 4)
-        for bank in range(2, 8):
-            if bank == 4:
-                quantise_wz()
-            if bank == 5:
-                project_z()
-            for half in range(2):
-                multiply(bank, 4 * half, 2)
-                if half == 1 and bank < 7:
-                    quantise_w(bank + 1)
-                multiply(bank, 4 * half + 2, 2)
-                if bank + 2 < 8:
-                    if half == 0 and bank % 2 == 0:
-                        group_w(bank + 2, 0, scopy)
-                    elif half == 0:
-                        shift_w(bank + 2, 0)
-                    else:
-                        shift_w(bank + 2, 1)
-                finish(*last)
-                last = (bank, 4 * half, 4)
-                if bank == 3 and half == 0:
-                    group_wz()
-        finish(*last, pieces=2)
+        turn_vectors()
+        group_wz()
+        quantise_w(3)
+        finish(0, 6, 2)
+        finish(1, 4, 4)
+        load_w(CHUNKS - 1, 0)
+        for chunk in range(1, CHUNKS):
+            first = 2 * chunk + 2
+            for pair in range(PAIRS):
+                if chunk == 2 and pair == 0:
+                    project_z()
+                if chunk == 2 and pair == 3:
+                    turn_z(0)
+                if chunk == 3 and pair == 0:
+                    turn_z(1)
+                project(chunk, pair)
+                if chunk == 2 and pair == 1:
+                    map_z(0)
+                    map_z(1)
+                if chunk + 1 < CHUNKS:
+                    if pair == 0:
+                        shift_w(first + 1, 1)
+                    elif pair == 1:
+                        shift_w(first + 1, 0)
+                    elif pair == 2:
+                        quantise_w(first)
+                        if chunk + 2 < CHUNKS:
+                            shift_w(first + 2, 1)
+                    elif pair == 3:
+                        quantise_w(first + 1)
+                        if chunk + 2 < CHUNKS:
+                            shift_w(first + 2, 0)
+                if chunk == 1 and pair == 1:
+                    quantise_wz()
+                if chunk < CHUNKS - 1:
+                    conclude(chunk, pair, 0, 2)
+                else:
+                    conclude(chunk, pair, 0, 1)
+                    conclude(chunk, pair, 1, 1, BANK if pair == PAIRS - 1 else CHUNK)

@@ -201,10 +201,10 @@ def tile_gaublock_pb_kernel(
                 in_=xn_grouped[pair][:].rearrange("p c r t -> p (c r t)"),
             )
 
-        def group_w(bank, c, copy):
+        def group_w(bank, c, copy, first=0, last=BANK):
             if bank not in w_grouped:
                 w_grouped[bank] = wstage.tile([P, PASSES, BANK, PACK], BF16, name="w_grouped", align_bytes=64)
-            regroup(copy, w_grouped[bank][:, c, :, :], columns(bank, c))
+            regroup(copy, w_grouped[bank][:, c, first:last, :], columns(bank, c)[:, :, first:last])
 
         def shift_w(bank, c):
             if bank not in w_grouped:
@@ -407,7 +407,7 @@ def tile_gaublock_pb_kernel(
         quantise_w(2)
         group_w(3, 0, scopy)
         finish(1, 0, 4)
-        shift_w(4, 0)
+        group_w(4, 0, scopy)
         multiply(0, 6, 2, 2)
         multiply(1, 6, 2)
         turn_vectors()
@@ -419,30 +419,29 @@ def tile_gaublock_pb_kernel(
         for chunk in range(1, CHUNKS):
             first = 2 * chunk + 2
             for pair in range(PAIRS):
-                if chunk == 2 and pair == 0:
+                if chunk == 1 and pair == 2:
                     project_z()
-                if chunk == 2 and pair == 3:
-                    turn_z(0)
-                if chunk == 3 and pair == 0:
-                    turn_z(1)
+                if chunk == 2 and pair in (1, 3):
+                    turn_z(pair // 2)
                 project(chunk, pair)
-                if chunk == 2 and pair == 1:
+                if chunk == 1 and pair == 3:
                     map_z(0)
                     map_z(1)
                 if chunk + 1 < CHUNKS:
                     if pair == 0:
                         shift_w(first + 1, 1)
                     elif pair == 1:
-                        shift_w(first + 1, 0)
+                        group_w(first + 1, 0, scopy, 0, BANK // 2)
                     elif pair == 2:
+                        group_w(first + 1, 0, vcopy, BANK // 2, BANK)
                         quantise_w(first)
                         if chunk + 2 < CHUNKS:
                             shift_w(first + 2, 1)
                     elif pair == 3:
                         quantise_w(first + 1)
                         if chunk + 2 < CHUNKS:
-                            shift_w(first + 2, 0)
-                if chunk == 1 and pair == 1:
+                            group_w(first + 2, 0, scopy)
+                if chunk == 1 and pair == 0:
                     quantise_wz()
                 if chunk < CHUNKS - 1:
                     conclude(chunk, pair, 0, 2)

@@ -41,11 +41,11 @@ def tile_gaublock_pb_kernel(
     with ExitStack() as ctx:
         keep = ctx.enter_context(tc.tile_pool(name="keep", bufs=1))
         stat = ctx.enter_context(tc.tile_pool(name="stat", bufs=4))
-        normed = ctx.enter_context(tc.tile_pool(name="normed", bufs=5))
+        normed = ctx.enter_context(tc.tile_pool(name="normed", bufs=4))
         raw = ctx.enter_context(tc.tile_pool(name="raw", bufs=5))
         stage = ctx.enter_context(tc.tile_pool(name="stage", bufs=2))
         wstage = ctx.enter_context(tc.tile_pool(name="wstage", bufs=3))
-        result = ctx.enter_context(tc.tile_pool(name="result", bufs=5))
+        result = ctx.enter_context(tc.tile_pool(name="result", bufs=6))
         psum = ctx.enter_context(tc.psum_pool(name="psum", bufs=8))
 
         ctx.enter_context(tc.manual_schedule())
@@ -206,13 +206,13 @@ def tile_gaublock_pb_kernel(
                 w_grouped[bank] = wstage.tile([P, PASSES, BANK, PACK], BF16, name="w_grouped", align_bytes=64)
             regroup(copy, w_grouped[bank][:, c, first:last, :], columns(bank, c)[:, :, first:last])
 
-        def shift_w(bank, c):
+        def shift_w(bank, c, first=0, last=BANK):
             if bank not in w_grouped:
                 w_grouped[bank] = wstage.tile([P, PASSES, BANK, PACK], BF16, name="w_grouped", align_bytes=64)
-            for a in range(4):
+            for a in range(first // 64, last // 64):
                 nc.gpsimd.tensor_scalar(
-                    out=w_grouped[bank][:, c, P * a : P * (a + 1), :],
-                    in0=columns(bank, c)[:, :, P * a : P * (a + 1)].rearrange("p t n -> p n t"),
+                    out=w_grouped[bank][:, c, 64 * a : 64 * (a + 1), :],
+                    in0=columns(bank, c)[:, :, 64 * a : 64 * (a + 1)].rearrange("p t n -> p n t"),
                     scalar1=1.0,
                     scalar2=0.0,
                     op0=ALU.mult,
@@ -277,9 +277,9 @@ def tile_gaublock_pb_kernel(
                 rows = slice(2 * pair + first, 2 * pair + first + count)
                 nc.sync.dma_start(out=uv_rows[(CHUNK * chunk) // E][:, rows, base : base + width], in_=part)
 
-        wz_grouped = keep.tile([P, PASSES, S, PACK], BF16, name="wz_grouped", align_bytes=64)
-
         def group_wz():
+            wz_grouped = stage.tile([P, PASSES, S, PACK], BF16, name="wz_grouped", tag="xn_grouped", align_bytes=64)
+            w_grouped["z"] = wz_grouped
             for c in range(PASSES):
                 regroup(nc.scalar.copy, wz_grouped[:, c, :, :], wz_raw[:, c, :, :])
 
@@ -287,7 +287,7 @@ def tile_gaublock_pb_kernel(
             nc.vector.quantize_mx(
                 out=wz_codes[:].rearrange("p c n -> p (c n)").bitcast(FP8X4),
                 scales=wz_scales[:].rearrange("p c n -> p (c n)"),
-                in_=wz_grouped[:].rearrange("p c n t -> p (c n t)"),
+                in_=w_grouped["z"][:].rearrange("p c n t -> p (c n t)"),
             )
 
         z_tiles = {}
@@ -340,7 +340,7 @@ def tile_gaublock_pb_kernel(
                     nc.tensor.transpose(
                         out=turned[:, b, :], in_=z_tiles[w][:, P * m : P * (m + 1)], identity=ident[:]
                     )
-                nc.scalar.copy(out=rows[:, 4 * a : 4 * (a + 1), :], in_=turned[:])
+                nc.vector.tensor_copy(out=rows[:, 4 * a : 4 * (a + 1), :], in_=turned[:])
             nc.sync.dma_start(out=qk_rows[w], in_=rows[:])
 
         g_cols = keep.tile([P, K_TILES], F32, name="g_cols")
@@ -357,11 +357,11 @@ def tile_gaublock_pb_kernel(
         group_w(0, 0, scopy)
         measure(2)
         invert(0)
-        normalise(0)
+        group_w(0, 1, scopy)
         measure(3)
+        normalise(0)
         merge(2)
         merge(3)
-        group_w(0, 1, scopy)
         turn(0)
         measure(4)
         invert(1)
@@ -419,11 +419,11 @@ def tile_gaublock_pb_kernel(
         for chunk in range(1, CHUNKS):
             first = 2 * chunk + 2
             for pair in range(PAIRS):
-                if chunk == 1 and pair == 2:
-                    project_z()
                 if chunk == 2 and pair in (1, 3):
                     turn_z(pair // 2)
                 project(chunk, pair)
+                if chunk == 1 and pair == 1:
+                    project_z()
                 if chunk == 1 and pair == 3:
                     map_z(0)
                     map_z(1)
@@ -433,7 +433,7 @@ def tile_gaublock_pb_kernel(
                     elif pair == 1:
                         group_w(first + 1, 0, scopy, 0, BANK // 2)
                     elif pair == 2:
-                        group_w(first + 1, 0, vcopy, BANK // 2, BANK)
+                        shift_w(first + 1, 0, BANK // 2, BANK)
                         quantise_w(first)
                         if chunk + 2 < CHUNKS:
                             shift_w(first + 2, 1)

@@ -206,13 +206,13 @@ def tile_gaublock_pb_kernel(
                 w_grouped[bank] = wstage.tile([P, PASSES, BANK, PACK], BF16, name="w_grouped", align_bytes=64)
             regroup(copy, w_grouped[bank][:, c, first:last, :], columns(bank, c)[:, :, first:last])
 
-        def shift_w(bank, c, first=0, last=BANK):
+        def shift_w(bank, c):
             if bank not in w_grouped:
                 w_grouped[bank] = wstage.tile([P, PASSES, BANK, PACK], BF16, name="w_grouped", align_bytes=64)
-            for a in range(first // 64, last // 64):
+            for a in range(4):
                 nc.gpsimd.tensor_scalar(
-                    out=w_grouped[bank][:, c, 64 * a : 64 * (a + 1), :],
-                    in0=columns(bank, c)[:, :, 64 * a : 64 * (a + 1)].rearrange("p t n -> p n t"),
+                    out=w_grouped[bank][:, c, P * a : P * (a + 1), :],
+                    in0=columns(bank, c)[:, :, P * a : P * (a + 1)].rearrange("p t n -> p n t"),
                     scalar1=1.0,
                     scalar2=0.0,
                     op0=ALU.mult,
@@ -340,7 +340,7 @@ def tile_gaublock_pb_kernel(
                     nc.tensor.transpose(
                         out=turned[:, b, :], in_=z_tiles[w][:, P * m : P * (m + 1)], identity=ident[:]
                     )
-                nc.vector.tensor_copy(out=rows[:, 4 * a : 4 * (a + 1), :], in_=turned[:])
+                nc.scalar.copy(out=rows[:, 4 * a : 4 * (a + 1), :], in_=turned[:])
             nc.sync.dma_start(out=qk_rows[w], in_=rows[:])
 
         g_cols = keep.tile([P, K_TILES], F32, name="g_cols")
@@ -429,11 +429,11 @@ def tile_gaublock_pb_kernel(
                     map_z(1)
                 if chunk + 1 < CHUNKS:
                     if pair == 0:
-                        shift_w(first + 1, 1)
+                        group_w(first + 1, 1, vcopy)
                     elif pair == 1:
                         group_w(first + 1, 0, scopy, 0, BANK // 2)
                     elif pair == 2:
-                        shift_w(first + 1, 0, BANK // 2, BANK)
+                        group_w(first + 1, 0, vcopy, BANK // 2, BANK)
                         quantise_w(first)
                         if chunk + 2 < CHUNKS:
                             shift_w(first + 2, 1)

from contextlib import ExitStack

import concourse.mybir as mybir
from concourse.masks import make_identity

F32 = mybir.dt.float32
BF16 = mybir.dt.bfloat16
U32 = mybir.dt.uint32
U8 = mybir.dt.uint8
FP8X4 = mybir.dt.float8_e4m3fn_x4
ALU = mybir.AluOpType
ACT = mybir.ActivationFunctionType

P = 128
PACK = 4
PASSES = 2
ROWS = 1024
D = 1024
E = 2048
S = 128
F = E + E + S
ROW_TILES = ROWS // P
PAIRS = ROW_TILES // 2
K_TILES = D // P
BANK = 512
CHUNK = 1024
CHUNKS = (E + E) // CHUNK
LN_EPS = 1e-5
FLOPS = 2 * ROWS * D * F


def tile_gaublock_pb_kernel(
    tc, x, ln_g, ln_b, W_in, b_in, gamma_q, beta_q, gamma_k, beta_k, out_0, out_1, out_2, out_3
):
    nc = tc.nc
    x_rows = x.flatten_outer_dims().rearrange("(p m) k -> p m k", m=ROW_TILES)
    w_rows = W_in.rearrange("(c p t) n -> p c t n", p=P, t=PACK)
    uv_rows = [out.flatten_outer_dims().rearrange("(p m) f -> p m f", m=ROW_TILES) for out in (out_0, out_1)]
    qk_rows = [out.flatten_outer_dims().rearrange("(p m) s -> p m s", m=ROW_TILES) for out in (out_2, out_3)]

    with ExitStack() as ctx:
        keep = ctx.enter_context(tc.tile_pool(name="keep", bufs=1))
        stat = ctx.enter_context(tc.tile_pool(name="stat", bufs=4))
        normed = ctx.enter_context(tc.tile_pool(name="normed", bufs=4))
        raw = ctx.enter_context(tc.tile_pool(name="raw", bufs=5))
        stage = ctx.enter_context(tc.tile_pool(name="stage", bufs=2))
        wstage = ctx.enter_context(tc.tile_pool(name="wstage", bufs=3))
        result = ctx.enter_context(tc.tile_pool(name="result", bufs=6))
        psum = ctx.enter_context(tc.psum_pool(name="psum", bufs=8))

        ctx.enter_context(tc.manual_schedule())

        g_raw = keep.tile([P, PASSES, PACK], BF16, name="g_raw")
        b_raw = keep.tile([P, PASSES, PACK], BF16, name="b_raw")
        nc.scalar.dma_start(out=g_raw[:], in_=ln_g.rearrange("(c p t) -> p c t", p=P, t=PACK))
        nc.scalar.dma_start(out=b_raw[:], in_=ln_b.rearrange("(c p t) -> p c t", p=P, t=PACK))
        minus_half = keep.tile([P, 2], F32, name="minus_half")
        nc.vector.memset(minus_half[:], -0.5)
        warm = keep.tile([P, 1], F32, name="warm")
        nc.scalar.activation(out=warm[:], in_=minus_half[:, 0:1], func=ACT.Silu)
        ident = keep.tile([P, P], F32, name="ident")
        make_identity(nc, ident[:])
        ident_bf16 = keep.tile([P, P], BF16, name="ident_bf16")
        nc.gpsimd.tensor_copy(out=ident_bf16[:], in_=ident[:])

        x_sb = keep.tile([P, ROW_TILES, D], BF16, name="x_sb")
        bias_all = keep.tile([P, E + E], BF16, name="bias_all")
        wz_raw = keep.tile([P, PASSES, PACK, S], BF16, name="wz_raw")
        w_raw, w_half = {}, {}

        def load_x(pair):
            nc.sync.dma_start(out=x_sb[:, 2 * pair : 2 * pair + 2, :], in_=x_rows[:, 2 * pair : 2 * pair + 2, :])

        def load_w(chunk, c):
            w_raw[(chunk, c)] = raw.tile([P, PACK, CHUNK], BF16, name="w_raw")
            nc.sync.dma_start(out=w_raw[(chunk, c)][:], in_=w_rows[:, c, :, CHUNK * chunk : CHUNK * (chunk + 1)])

        def load_half(h, c):
            w_half[(h, c)] = keep.tile([P, PACK, BANK], BF16, name="w_half%d_%d" % (h, c))
            nc.sync.dma_start(out=w_half[(h, c)][:], in_=w_rows[:, c, :, BANK * h : BANK * (h + 1)])

        def columns(bank, c):
            chunk, h = divmod(bank, CHUNK // BANK)
            if chunk == 0:
                return w_half[(h, c)][:]
            return w_raw[(chunk, c)][:, :, BANK * h : BANK * (h + 1)]

        for m in range(2):
            nc.sync.dma_start(out=x_sb[:, m : m + 1, :], in_=x_rows[:, m : m + 1, :])
        load_half(0, 0)
        load_x(1)
        load_half(0, 1)
        load_x(2)
        load_x(3)
        load_half(1, 0)
        load_half(1, 1)
        nc.sync.dma_start(out=bias_all[:], in_=b_in[0 : E + E].partition_broadcast(P))
        for chunk in range(1, CHUNKS - 1):
            for c in range(PASSES):
                load_w(chunk, c)
        load_w(CHUNKS - 1, 1)
        for c in range(PASSES):
            nc.sync.dma_start(out=wz_raw[:, c, :, :], in_=w_rows[:, c, :, 2 * E : F])
        z_rows = keep.tile([P, S], BF16, name="z_rows")
        nc.gpsimd.memset(z_rows[:], 0.0)
        for i, vec in enumerate((b_in[E + E : F], gamma_q, beta_q, gamma_k, beta_k)):
            nc.sync.dma_start(out=z_rows[i : i + 1, :], in_=vec.unsqueeze(0))
        z_cols = keep.tile([P, 8], F32, name="z_cols")

        xn_codes = keep.tile([P, PAIRS, PASSES, 2 * P], U32, name="xn_codes", align_bytes=64)
        xn_scales = keep.tile([P, PAIRS, PASSES, 2 * P], U8, name="xn_scales", align_bytes=64)
        w_codes = keep.tile([P, 2 * E // BANK, PASSES, BANK], U32, name="w_codes", align_bytes=64)
        w_scales = keep.tile([P, 2 * E // BANK, PASSES, BANK], U8, name="w_scales", align_bytes=64)
        wz_codes = keep.tile([P, PASSES, S], U32, name="wz_codes", align_bytes=64)
        wz_scales = keep.tile([P, PASSES, S], U8, name="wz_scales", align_bytes=64)

        def regroup(copy, dst, src):
            copy(
                out=dst.rearrange("p (a i) t -> p a t i", i=4),
                in_=src.rearrange("p t (a i) -> p a t i", i=4),
            )

        half_stats, mean_var, rstds, y_rows, k_tiles, xn_grouped, w_grouped = {}, {}, {}, {}, {}, {}, {}

        def measure(m):
            pair, i = divmod(m, 2)
            if i == 0:
                mean_var[pair] = stat.tile([P, 2, 2], F32, name="mean_var")
            stats = stat.tile([P, 2, 6], F32, name="stats")
            half_stats[m] = stats
            for h in range(2):
                nc.vector.bn_stats(out=stats[:, h, :], in_=x_sb[:, m, 512 * h : 512 * (h + 1)])

        def merge(m):
            pair, i = divmod(m, 2)
            nc.vector.bn_aggr(out=mean_var[pair][:, i, :], in_=half_stats[m][:].rearrange("p a b -> p (a b)"))

        def invert(pair):
            var_eps = stat.tile([P, 2], F32, name="var_eps")
            nc.vector.tensor_scalar_add(out=var_eps[:], in0=mean_var[pair][:, :, 1], scalar1=LN_EPS)
            rstds[pair] = stat.tile([P, 2], F32, name="rstd")
            nc.gpsimd.tensor_tensor(out=rstds[pair][:], in0=var_eps[:], in1=minus_half[:], op=ALU.pow)

        def normalise(pair):
            means, rstd = mean_var[pair], rstds[pair]
            shift = stat.tile([P, 1], F32, name="shift")
            nc.vector.scalar_tensor_tensor(
                out=shift[:], in0=means[:, 1, 0:1], scalar=-1.0, in1=rstd[:, 1:2], op0=ALU.mult, op1=ALU.mult
            )
            for i in range(2):
                y = normed.tile([P, PASSES, PACK, P], F32, name="y")
                y_rows[(pair, i)] = y
                x_k = x_sb[:, 2 * pair + i, :].rearrange("p (c q t) -> p c t q", c=PASSES, t=PACK)
                if i == 0:
                    nc.vector.tensor_scalar(
                        out=y[:],
                        in0=x_k,
                        scalar1=means[:, i, 0:1],
                        scalar2=rstd[:, i : i + 1],
                        op0=ALU.subtract,
                        op1=ALU.mult,
                    )
                else:
                    nc.scalar.activation(out=y[:], in_=x_k, func=ACT.Identity, scale=rstd[:, 1:2], bias=shift[:])

        def turn(pair):
            k_tiles[pair] = stage.tile([P, K_TILES, 2 * P], BF16, name="k_tiles")
            for a in range(K_TILES // 2):
                turned = psum.tile([P, 2, 2 * P], F32, name="turned", tag="bank")
                for b in range(2):
                    j = 2 * a + b
                    for i in range(2):
                        nc.tensor.transpose(
                            out=turned[:, b, P * i : P * (i + 1)],
                            in_=y_rows[(pair, i)][:, j // PACK, j % PACK, :],
                            identity=ident[:],
                        )
                for b in range(2):
                    j = 2 * a + b
                    nc.scalar.activation(
                        out=k_tiles[pair][:, j, :],
                        in_=turned[:, b, :],
                        func=ACT.Identity,
                        scale=g_cols[:, j : j + 1],
                        bias=b_cols[:, j : j + 1],
                    )

        def group_x(pair):
            xn_grouped[pair] = stage.tile([P, PASSES, 2 * P, PACK], BF16, name="xn_grouped", align_bytes=64)
            for c in range(PASSES):
                regroup(
                    nc.vector.tensor_copy,
                    xn_grouped[pair][:, c, :, :],
                    k_tiles[pair][:, PACK * c : PACK * (c + 1), :],
                )

        def quantise_x(pair):
            nc.vector.quantize_mx(
                out=xn_codes[:, pair, :, :].rearrange("p c r -> p (c r)").bitcast(FP8X4),
                scales=xn_scales[:, pair, :, :].rearrange("p c r -> p (c r)"),
                in_=xn_grouped[pair][:].rearrange("p c r t -> p (c r t)"),
            )

        def group_w(bank, c, copy, first=0, last=BANK):
            if bank not in w_grouped:
                w_grouped[bank] = wstage.tile([P, PASSES, BANK, PACK], BF16, name="w_grouped", align_bytes=64)
            regroup(copy, w_grouped[bank][:, c, first:last, :], columns(bank, c)[:, :, first:last])

        def shift_w(bank, c):
            if bank not in w_grouped:
                w_grouped[bank] = wstage.tile([P, PASSES, BANK, PACK], BF16, name="w_grouped", align_bytes=64)
            for a in range(4):
                nc.gpsimd.tensor_scalar(
                    out=w_grouped[bank][:, c, P * a : P * (a + 1), :],
                    in0=columns(bank, c)[:, :, P * a : P * (a + 1)].rearrange("p t n -> p n t"),
                    scalar1=1.0,
                    scalar2=0.0,
                    op0=ALU.mult,
                    op1=ALU.add,
                )

        def quantise_w(bank):
            nc.vector.quantize_mx(
                out=w_codes[:, bank, :, :].rearrange("p c n -> p (c n)").bitcast(FP8X4),
                scales=w_scales[:, bank, :, :].rearrange("p c n -> p (c n)"),
                in_=w_grouped[bank][:].rearrange("p c n t -> p (c n t)"),
            )

        def mx_group(acc, tile_m, rhs_codes, rhs_scales):
            pair, i = tile_m // 2, tile_m % 2
            for c in range(PASSES):
                nc.tensor.matmul_mx(
                    out=acc,
                    lhsT=xn_codes[:, pair, c, P * i : P * (i + 1)].bitcast(FP8X4),
                    lhsT_scale=xn_scales[:, pair, c, P * i : P * (i + 1)],
                    rhs=rhs_codes[:, c, :].bitcast(FP8X4),
                    rhs_scale=rhs_scales[:, c, :],
                    start=(c == 0),
                    stop=(c == PASSES - 1),
                )

        outs = {}

        def add_bias(out, tile_m, bank):
            acc = psum.tile([P, BANK], F32, name="acc", tag="bank")
            mx_group(acc[:], tile_m, w_codes[:, bank, :, :], w_scales[:, bank, :, :])
            nc.vector.tensor_tensor(out=out, in0=acc[:], in1=bias_all[:, BANK * bank : BANK * (bank + 1)], op=ALU.add)

        def multiply(bank, first, count, tiles=4):
            key = (bank, first // tiles * tiles, tiles)
            if key not in outs:
                outs[key] = result.tile([P, tiles, BANK], F32, name="out_sb")
            for i in range(count):
                add_bias(outs[key][:, (first + i) % tiles, :], first + i, bank)

        def finish(bank, first, count):
            out_sb = outs[(bank, first, count)]
            col = (BANK * bank) % E
            nc.scalar.activation(out=out_sb[:], in_=out_sb[:], func=ACT.Silu)
            nc.sync.dma_start(
                out=uv_rows[(BANK * bank) // E][:, first : first + count, col : col + BANK], in_=out_sb[:]
            )

        def project(chunk, pair):
            out_sb = result.tile([P, 2, CHUNK], F32, name="out_sb")
            outs[(chunk, pair)] = out_sb
            halves = range(CHUNK // BANK)
            order = [(i, h) for i in range(2) for h in halves] if chunk == CHUNKS - 1 else [(i, h) for h in halves for i in range(2)]
            for i, h in order:
                add_bias(out_sb[:, i, BANK * h : BANK * (h + 1)], 2 * pair + i, CHUNK // BANK * chunk + h)

        def conclude(chunk, pair, first, count, width=CHUNK):
            for col in range(0, CHUNK, width):
                part = outs[(chunk, pair)][:, first : first + count, col : col + width]
                nc.scalar.activation(out=part, in_=part, func=ACT.Silu)
                base = (CHUNK * chunk) % E + col
                rows = slice(2 * pair + first, 2 * pair + first + count)
                nc.sync.dma_start(out=uv_rows[(CHUNK * chunk) // E][:, rows, base : base + width], in_=part)

        def group_wz():
            wz_grouped = stage.tile([P, PASSES, S, PACK], BF16, name="wz_grouped", tag="xn_grouped", align_bytes=64)
            w_grouped["z"] = wz_grouped
            for c in range(PASSES):
                regroup(nc.scalar.copy, wz_grouped[:, c, :, :], wz_raw[:, c, :, :])

        def quantise_wz():
            nc.vector.quantize_mx(
                out=wz_codes[:].rearrange("p c n -> p (c n)").bitcast(FP8X4),
                scales=wz_scales[:].rearrange("p c n -> p (c n)"),
                in_=w_grouped["z"][:].rearrange("p c n t -> p (c n t)"),
            )

        z_tiles = {}

        def turn_vectors():
            cols = psum.tile([P, S], F32, name="z_turned", tag="bank")
            nc.tensor.matmul(out=cols[:], lhsT=z_rows[:], rhs=ident_bf16[:], start=True, stop=True)
            nc.scalar.copy(out=z_cols[:], in_=cols[:, 0:8])

        def project_z():
            z_t = normed.tile([P, ROWS], F32, name="z_t", tag="y")
            z_tiles["z"] = z_t
            for a in range(2):
                acc = psum.tile([P, 2, 2 * P], F32, name="acc_z", tag="bank")
                for b in range(2):
                    for c in range(PASSES):
                        nc.tensor.matmul_mx(
                            out=acc[:, b, :],
                            lhsT=wz_codes[:, c, :].bitcast(FP8X4),
                            lhsT_scale=wz_scales[:, c, :],
                            rhs=xn_codes[:, 2 * a + b, c, :].bitcast(FP8X4),
                            rhs_scale=xn_scales[:, 2 * a + b, c, :],
                            start=(c == 0),
                            stop=(c == PASSES - 1),
                        )
                nc.scalar.activation(
                    out=z_t[:, BANK * a : BANK * (a + 1)],
                    in_=acc[:].rearrange("p b r -> p (b r)"),
                    func=ACT.Silu,
                    bias=z_cols[:, 0:1],
                )

        def map_z(w):
            z_tiles[w] = normed.tile([P, ROWS], F32, name="m_t", tag="y")
            nc.vector.tensor_scalar(
                out=z_tiles[w][:],
                in0=z_tiles["z"][:],
                scalar1=z_cols[:, 2 * w + 1 : 2 * w + 2],
                scalar2=z_cols[:, 2 * w + 2 : 2 * w + 3],
                op0=ALU.mult,
                op1=ALU.add,
            )

        def turn_z(w):
            rows = normed.tile([P, ROW_TILES, S], F32, name="rows", tag="y")
            for a in range(2):
                turned = psum.tile([P, 4, S], F32, name="turned_z", tag="bank")
                for b in range(4):
                    m = 4 * a + b
                    nc.tensor.transpose(
                        out=turned[:, b, :], in_=z_tiles[w][:, P * m : P * (m + 1)], identity=ident[:]
                    )
                nc.scalar.copy(out=rows[:, 4 * a : 4 * (a + 1), :], in_=turned[:])
            nc.sync.dma_start(out=qk_rows[w], in_=rows[:])

        g_cols = keep.tile([P, K_TILES], F32, name="g_cols")
        b_cols = keep.tile([P, K_TILES], F32, name="b_cols")
        banks = 2 * E // BANK

        vcopy, scopy = nc.vector.tensor_copy, nc.scalar.copy
        measure(0)
        measure(1)
        merge(0)
        merge(1)
        nc.gpsimd.tensor_copy(out=g_cols[:], in_=g_raw[:].rearrange("p c t -> p (c t)"))
        nc.gpsimd.tensor_copy(out=b_cols[:], in_=b_raw[:].rearrange("p c t -> p (c t)"))
        group_w(0, 0, scopy)
        measure(2)
        invert(0)
        group_w(0, 1, scopy)
        measure(3)
        normalise(0)
        merge(2)
        merge(3)
        turn(0)
        measure(4)
        invert(1)
        quantise_w(0)
        measure(5)
        normalise(1)
        merge(4)
        merge(5)
        group_x(0)
        measure(6)
        invert(2)
        quantise_x(0)
        group_w(1, 0, scopy)
        turn(1)
        measure(7)
        merge(6)
        normalise(2)
        merge(7)
        invert(3)
        multiply(0, 0, 2, 2)
        group_x(1)
        group_w(1, 1, vcopy)
        quantise_x(1)
        finish(0, 0, 2)
        turn(2)
        normalise(3)
        multiply(0, 2, 2, 2)
        group_x(2)
        quantise_w(1)
        group_w(2, 0, scopy)
        turn(3)
        quantise_x(2)
        group_w(3, 1, vcopy)
        finish(0, 2, 2)
        multiply(0, 4, 2, 2)
        multiply(1, 0, 4)
        group_w(2, 1, scopy)
        finish(0, 4, 2)
        group_x(3)
        shift_w(4, 1)
        multiply(1, 4, 2)
        quantise_x(3)
        quantise_w(2)
        group_w(3, 0, scopy)
        finish(1, 0, 4)
        group_w(4, 0, scopy)
        multiply(0, 6, 2, 2)
        multiply(1, 6, 2)
        turn_vectors()
        group_wz()
        quantise_w(3)
        finish(0, 6, 2)
        finish(1, 4, 4)
        load_w(CHUNKS - 1, 0)
        for chunk in range(1, CHUNKS):
            first = 2 * chunk + 2
            for pair in range(PAIRS):
                if chunk == 2 and pair in (1, 3):
                    turn_z(pair // 2)
                project(chunk, pair)
                if chunk == 1 and pair == 1:
                    project_z()
                if chunk == 1 and pair == 3:
                    map_z(0)
                    map_z(1)
                if chunk + 1 < CHUNKS:
                    if pair == 0:
                        group_w(first + 1, 1, vcopy)
                    elif pair == 1:
                        group_w(first + 1, 0, scopy, 0, BANK // 2)
                    elif pair == 2:
                        group_w(first + 1, 0, vcopy, BANK // 2, BANK)
                        quantise_w(first)
                        if chunk + 2 < CHUNKS:
                            shift_w(first + 2, 1)
                    elif pair == 3:
                        quantise_w(first + 1)
                        if chunk + 2 < CHUNKS:
                            group_w(first + 2, 0, scopy)
                if chunk == 1 and pair == 0:
                    quantise_wz()
                if chunk < CHUNKS - 1:
                    conclude(chunk, pair, 0, 2)
                else:
                    conclude(chunk, pair, 0, 1)
                    conclude(chunk, pair, 1, 1, BANK if pair == PAIRS - 1 else CHUNK)
